import numpy as np
import ml_dtypes


def mxq(x, axis, fmt="e4m3"):
    dtype, down = {"e4m3": (ml_dtypes.float8_e4m3fn, 7), "e5m2": (ml_dtypes.float8_e5m2, 14)}[fmt]
    v = np.moveaxis(np.asarray(x, np.float32).astype(ml_dtypes.bfloat16).astype(np.float64), axis, -1)
    blocks = v.reshape(v.shape[:-1] + (-1, 32))
    amax = np.abs(blocks).max(-1, keepdims=True)
    byte = np.maximum(np.where(amax > 0, np.frexp(amax)[1] - 1 + 127, 0) - down, 1)
    scale = np.exp2(byte - 127.0)
    codes = (blocks / scale).astype(np.float32).astype(dtype).astype(np.float64)
    return np.moveaxis((codes * scale).reshape(v.shape), -1, axis)


WIDE = False


def mx_kscale(k):
    if not WIDE:
        return np.ones(k)
    levels = np.array([10, -10, 5, -5, 0])
    a = np.random.permutation(np.resize(levels, k // 512 * 4)).reshape(k // 512, 4)
    idx = np.arange(k)
    return np.exp2(a[idx // 512, idx % 128 // 32])


BF16 = ml_dtypes.bfloat16


def bf(x):
    return np.asarray(x, np.float32).astype(BF16)


def f64(x):
    return np.asarray(x).astype(np.float64)


B, M, H_ENC, N, H_DEC = 512, 16384, 512, 128, 128
SNR = 25.0
NOISE_STD = float(np.sqrt(1.0 / (2.0 * 10.0 ** (SNR / 10.0))))


def setup_inputs():
    s = mx_kscale(M)
    t = mx_kscale(H_ENC)
    theta = np.random.uniform(0.3, 1.2)
    return {"x": bf(np.random.standard_normal((B, M)) * s),
            "noise": bf(np.random.standard_normal((B, N)) * NOISE_STD),
            "h": bf(np.array([np.cos(theta), np.sin(theta)])),
            "W1": bf(np.random.standard_normal((H_ENC, M)) / np.sqrt(M) / s[None, :] * t[:, None]),
            "b1": bf(np.random.standard_normal(H_ENC) * 0.3 * t),
            "W2": bf(np.random.standard_normal((N, H_ENC)) / np.sqrt(H_ENC) / t[None, :]),
            "b2": bf(np.random.standard_normal(N) * 0.3)}


def reference(x, noise, h, W1, b1, W2, b2):
    h = f64(h)
    a = np.maximum((mxq(f64(x), 1, "e4m3") @ mxq(f64(W1), 1, "e4m3").T) + f64(b1), 0.0)
    z = (mxq(a, 1, "e4m3") @ mxq(f64(W2), 1, "e4m3").T) + f64(b2)
    scale = np.sqrt(N * 0.5)
    z = scale * z / np.linalg.norm(z, axis=1, keepdims=True)
    zc = z.reshape(B, N // 2, 2)
    yr = zc[..., 0] * h[0] - zc[..., 1] * h[1]
    yi = zc[..., 0] * h[1] + zc[..., 1] * h[0]
    y = np.stack([yr, yi], axis=-1).reshape(B, N)
    return y + f64(noise)

@@ -1,0 +1,257 @@
+from contextlib import ExitStack
+
+import concourse.mybir as mybir
+from concourse.masks import make_identity
+
+BF16 = mybir.dt.bfloat16
+F32 = mybir.dt.float32
+U32 = mybir.dt.uint32
+U8 = mybir.dt.uint8
+FP8X4 = mybir.dt.float8_e4m3fn_x4
+ALU = mybir.AluOpType
+ACT = mybir.ActivationFunctionType
+
+P = 128
+PACK = 4
+K_PASS = P * PACK
+HALVES = 2
+
+BATCH, K1, HIDDEN, N_OUT = 512, 16384, 512, 128
+ROW_TILES = BATCH // P
+PASSES = K1 // K_PASS
+BANK_ROWS = 2 * P
+
+CHUNK_PASSES = 4
+CHUNK_K = CHUNK_PASSES * K_PASS
+CHUNKS = PASSES // CHUNK_PASSES
+RAW_BUFS = 4
+
+PASSES_PER_ROUND = 1
+ROUNDS = PASSES // PASSES_PER_ROUND
+
+FLOPS = 2 * BATCH * K1 * HIDDEN + 2 * BATCH * HIDDEN * N_OUT
+
+
+def doubling_pieces(total, first):
+    cuts = [(0, first)]
+    while cuts[-1][1] < total:
+        end = cuts[-1][1]
+        cuts.append((end, 2 * end))
+    return cuts
+
+
+def tile_channel_net_pa_k_kernel(tc, x, noise, h, W1, b1, W2, b2, out):
+    nc = tc.nc
+    with ExitStack() as ctx:
+        ctx.enter_context(tc.manual_schedule())
+        const = ctx.enter_context(tc.tile_pool(name="const", bufs=1))
+        raw_pool = ctx.enter_context(tc.tile_pool(name="raw", bufs=RAW_BUFS))
+        stage = ctx.enter_context(tc.tile_pool(name="stage", bufs=2 * PASSES_PER_ROUND))
+        tail = ctx.enter_context(tc.tile_pool(name="tail", bufs=1))
+        acc_pool = ctx.enter_context(tc.psum_pool(name="acc", bufs=1))
+        bank_pool = ctx.enter_context(tc.psum_pool(name="bank", bufs=4))
+
+        x_rows = x.rearrange("(p t) k -> p t k", t=ROW_TILES)
+        w1_rows = W1.rearrange("(p t) k -> p t k", t=ROW_TILES)
+
+        def load_chunk(c):
+            x_raw = raw_pool.tile([P, ROW_TILES, CHUNK_K], BF16)
+            w_raw = raw_pool.tile([P, ROW_TILES, CHUNK_K], BF16)
+            pieces = doubling_pieces(CHUNK_K, K_PASS) if c == 0 else [(0, CHUNK_K)]
+            for lo, hi in pieces:
+                k_range = slice(c * CHUNK_K + lo, c * CHUNK_K + hi)
+                nc.sync.dma_start(out=x_raw[:, :, lo:hi], in_=x_rows[:, :, k_range])
+                nc.sync.dma_start(out=w_raw[:, :, lo:hi], in_=w1_rows[:, :, k_range])
+            return x_raw, w_raw
+
+        chunks = {}
+        for c in range(RAW_BUFS):
+            chunks[c] = load_chunk(c)
+
+        w2_raw = const.tile([P, HIDDEN], BF16)
+        nc.sync.dma_start(out=w2_raw[:], in_=W2)
+        b1_raw = const.tile([P, PACK], BF16)
+        nc.sync.dma_start(out=b1_raw[:], in_=b1.rearrange("(p t) -> p t", t=PACK))
+        h_raw = const.tile([P, 2], BF16)
+        nc.sync.dma_start(out=h_raw[:], in_=h.partition_broadcast(P))
+        b2_all = const.tile([P, N_OUT], BF16)
+        nc.sync.dma_start(out=b2_all[:], in_=b2.partition_broadcast(P))
+        noise_sb = const.tile([P, ROW_TILES, N_OUT], BF16)
+        nc.sync.dma_start(out=noise_sb[:], in_=noise.rearrange("(p t) n -> p t n", t=ROW_TILES))
+
+        one = const.tile([P, 1], F32)
+        nc.vector.memset(one[:], 1.0)
+        nc.scalar.activation(out=one[:], in_=one[:], func=ACT.Sqrt)
+
+        ident = const.tile([P, P], F32)
+        make_identity(nc, ident[:])
+        b1_f = const.tile([P, PACK], F32)
+        nc.gpsimd.tensor_copy(out=b1_f[:], in_=b1_raw[:])
+        h_f = const.tile([P, 2], F32)
+        nc.gpsimd.tensor_copy(out=h_f[:], in_=h_raw[:])
+        minus_h1 = const.tile([P, 1], F32)
+        nc.gpsimd.tensor_scalar(
+            out=minus_h1[:], in0=h_raw[:, 1:2], scalar1=-1.0, scalar2=0.0, op0=ALU.mult, op1=ALU.add
+        )
+
+        acc = [acc_pool.tile([P, BATCH], F32, name="acc%d" % t) for t in range(PACK)]
+
+        def k_onto_partitions(raw, g_in_chunk, grouped, copies):
+            words = raw[:].bitcast(F32)
+            grouped_words = grouped[:].bitcast(F32).rearrange("p (r u) -> p r u", u=HALVES)
+            first_word = g_in_chunk * (K_PASS // 2)
+            for bank in range(ROW_TILES * P // BANK_ROWS):
+                flipped = bank_pool.tile([P, HALVES, BANK_ROWS], F32, tag="bank")
+                for local in range(BANK_ROWS // P):
+                    row_tile = bank * (BANK_ROWS // P) + local
+                    for u in range(HALVES):
+                        nc.tensor.transpose(
+                            flipped[:, u, local * P : (local + 1) * P],
+                            words[:, row_tile, first_word + u * P : first_word + (u + 1) * P],
+                            ident[:],
+                        )
+                copies[bank](
+                    out=grouped_words[:, bank * BANK_ROWS : (bank + 1) * BANK_ROWS, :],
+                    in_=flipped[:].rearrange("p u r -> p r u"),
+                )
+
+        grouped_of = {}
+        packed_of = {}
+
+        def flip(g):
+            c, g_in_chunk = divmod(g, CHUNK_PASSES)
+            x_raw, w_raw = chunks[c]
+            x_grouped = stage.tile([P, BATCH * PACK], BF16, align_bytes=64)
+            w_grouped = stage.tile([P, HIDDEN * PACK], BF16, align_bytes=64)
+            k_onto_partitions(x_raw, g_in_chunk, x_grouped, [nc.vector.tensor_copy, nc.scalar.copy])
+            k_onto_partitions(w_raw, g_in_chunk, w_grouped, [nc.scalar.copy, nc.scalar.copy])
+            grouped_of[g] = (x_grouped, w_grouped)
+            if g_in_chunk == CHUNK_PASSES - 1 and c + RAW_BUFS < CHUNKS:
+                chunks[c + RAW_BUFS] = load_chunk(c + RAW_BUFS)
+
+        def quantise(g):
+            x_grouped, w_grouped = grouped_of[g]
+            x_codes = stage.tile([P, BATCH], U32, align_bytes=64)
+            x_scales = stage.tile([P, BATCH], U8, align_bytes=64)
+            w_codes = stage.tile([P, HIDDEN], U32, align_bytes=64)
+            w_scales = stage.tile([P, HIDDEN], U8, align_bytes=64)
+            nc.vector.quantize_mx(out=x_codes[:].bitcast(FP8X4), scales=x_scales[:], in_=x_grouped[:])
+            nc.vector.quantize_mx(out=w_codes[:].bitcast(FP8X4), scales=w_scales[:], in_=w_grouped[:])
+            packed_of[g] = (x_codes, x_scales, w_codes, w_scales)
+
+        def multiply(g):
+            x_codes, x_scales, w_codes, w_scales = packed_of[g]
+            for t in range(PACK):
+                units = slice(t * P, (t + 1) * P)
+                nc.tensor.matmul_mx(
+                    out=acc[t][:],
+                    lhsT=w_codes[:, units].bitcast(FP8X4),
+                    lhsT_scale=w_scales[:, units],
+                    rhs=x_codes[:].bitcast(FP8X4),
+                    rhs_scale=x_scales[:],
+                    start=(g == 0),
+                    stop=(g == PASSES - 1),
+                )
+
+        def passes_of(rnd):
+            return range(rnd * PASSES_PER_ROUND, (rnd + 1) * PASSES_PER_ROUND)
+
+        def flip_and_quantise_w2():
+            w2_words = w2_raw[:].bitcast(F32).rearrange("n (p u) -> n u p", u=HALVES)
+            w2_flipped = bank_pool.tile([P, HALVES, N_OUT], F32, tag="bank")
+            for u in range(HALVES):
+                nc.tensor.transpose(w2_flipped[:, u, :], w2_words[:, u, :], ident[:])
+            w2_grouped = const.tile([P, N_OUT * PACK], BF16, align_bytes=64)
+            nc.scalar.copy(
+                out=w2_grouped[:].bitcast(F32).rearrange("p (n u) -> p n u", u=HALVES),
+                in_=w2_flipped[:].rearrange("p u n -> p n u"),
+            )
+            w2_codes = const.tile([P, N_OUT], U32, align_bytes=64)
+            w2_scales = const.tile([P, N_OUT], U8, align_bytes=64)
+            nc.vector.quantize_mx(out=w2_codes[:].bitcast(FP8X4), scales=w2_scales[:], in_=w2_grouped[:])
+            return w2_codes, w2_scales
+
+        for g in passes_of(0):
+            flip(g)
+        for g in passes_of(0):
+            quantise(g)
+        for rnd in range(1, ROUNDS):
+            for g in passes_of(rnd):
+                flip(g)
+            for g in passes_of(rnd - 1):
+                multiply(g)
+            for g in passes_of(rnd):
+                quantise(g)
+        w2_codes, w2_scales = flip_and_quantise_w2()
+        for g in passes_of(ROUNDS - 1):
+            multiply(g)
+
+        a_planes = tail.tile([P, PACK, BATCH], BF16)
+        for t in range(PACK):
+            if t % 2 == 0:
+                nc.scalar.activation(
+                    out=a_planes[:, t, :], in_=acc[t][:], func=ACT.Relu, bias=b1_f[:, t : t + 1], scale=1.0
+                )
+            else:
+                nc.vector.tensor_scalar(
+                    out=a_planes[:, t, :], in0=acc[t][:], scalar1=b1_f[:, t : t + 1], scalar2=0.0,
+                    op0=ALU.add, op1=ALU.max,
+                )
+        a_grouped = tail.tile([P, BATCH, PACK], BF16, align_bytes=64)
+        nc.vector.tensor_copy(out=a_grouped[:], in_=a_planes[:].rearrange("p t b -> p b t"))
+        a_codes = tail.tile([P, BATCH], U32, align_bytes=64)
+        a_scales = tail.tile([P, BATCH], U8, align_bytes=64)
+        nc.vector.quantize_mx(
+            out=a_codes[:].bitcast(FP8X4), scales=a_scales[:], in_=a_grouped[:].rearrange("p b t -> p (b t)")
+        )
+
+        z_ps = bank_pool.tile([P, ROW_TILES, N_OUT], F32, tag="bank")
+        for t in range(ROW_TILES):
+            rows = slice(t * P, (t + 1) * P)
+            nc.tensor.matmul_mx(
+                out=z_ps[:, t, :],
+                lhsT=a_codes[:, rows].bitcast(FP8X4),
+                lhsT_scale=a_scales[:, rows],
+                rhs=w2_codes[:].bitcast(FP8X4),
+                rhs_scale=w2_scales[:],
+                start=True,
+                stop=True,
+            )
+
+        z = tail.tile([P, ROW_TILES, N_OUT], F32)
+        nc.vector.tensor_tensor(
+            out=z[:], in0=z_ps[:], in1=b2_all[:].unsqueeze(1).to_broadcast([P, ROW_TILES, N_OUT]), op=ALU.add
+        )
+        squares = tail.tile([P, ROW_TILES, N_OUT], F32)
+        sum_sq = tail.tile([P, ROW_TILES], F32)
+        for t in range(ROW_TILES):
+            nc.scalar.activation(
+                out=squares[:, t, :], in_=z[:, t, :], func=ACT.Square, accum_out=sum_sq[:, t : t + 1]
+            )
+        norm_by_8 = tail.tile([P, ROW_TILES], F32)
+        nc.scalar.activation(out=norm_by_8[:], in_=sum_sq[:], func=ACT.Sqrt, scale=2.0 / N_OUT)
+
+        z_h0 = tail.tile([P, ROW_TILES, N_OUT], F32)
+        turned = tail.tile([P, ROW_TILES, N_OUT], F32)
+        nc.vector.tensor_scalar(out=z_h0[:], in0=z[:], scalar1=h_f[:, 0:1], scalar2=None, op0=ALU.mult)
+        z_pairs = z[:].rearrange("p t (j c) -> p (t j) c", c=2)
+        z_h0_pairs = z_h0[:].rearrange("p t (j c) -> p (t j) c", c=2)
+        turned_pairs = turned[:].rearrange("p t (j c) -> p (t j) c", c=2)
+        nc.vector.scalar_tensor_tensor(
+            out=turned_pairs[:, :, 0], in0=z_pairs[:, :, 1], scalar=minus_h1[:, 0:1], in1=z_h0_pairs[:, :, 0],
+            op0=ALU.mult, op1=ALU.add,
+        )
+        nc.vector.scalar_tensor_tensor(
+            out=turned_pairs[:, :, 1], in0=z_pairs[:, :, 0], scalar=h_f[:, 1:2], in1=z_h0_pairs[:, :, 1],
+            op0=ALU.mult, op1=ALU.add,
+        )
+
+        gain = tail.tile([P, ROW_TILES], F32)
+        nc.vector.reciprocal(out=gain[:], in_=norm_by_8[:])
+        y = tail.tile([P, ROW_TILES, N_OUT], F32)
+        for t in range(ROW_TILES):
+            nc.vector.scalar_tensor_tensor(
+                out=y[:, t, :], in0=turned[:, t, :], scalar=gain[:, t : t + 1], in1=noise_sb[:, t, :],
+                op0=ALU.mult, op1=ALU.add,
+            )
+        nc.sync.dma_start(out=out.rearrange("(p t) n -> p t n", t=ROW_TILES), in_=y[:])

@@ -26,7 +26,7 @@ CHUNK_K = CHUNK_PASSES * K_PASS
 CHUNKS = PASSES // CHUNK_PASSES
 RAW_BUFS = 4
 
-PASSES_PER_ROUND = 1
+PASSES_PER_ROUND = 2
 ROUNDS = PASSES // PASSES_PER_ROUND
 
 FLOPS = 2 * BATCH * K1 * HIDDEN + 2 * BATCH * HIDDEN * N_OUT

@@ -21,13 +21,18 @@ ROW_TILES = BATCH // P
 PASSES = K1 // K_PASS
 BANK_ROWS = 2 * P
 
-CHUNK_PASSES = 4
+CHUNK_PASSES = 2
 CHUNK_K = CHUNK_PASSES * K_PASS
 CHUNKS = PASSES // CHUNK_PASSES
-RAW_BUFS = 4
+RAW_BUFS = 8
 
-PASSES_PER_ROUND = 2
+PASSES_PER_ROUND = 1
 ROUNDS = PASSES // PASSES_PER_ROUND
+
+PAIRS = N_OUT // 2
+SIDES = 2
+SIDE_TILES = ROW_TILES // SIDES
+SIDE_ROWS = SIDE_TILES * P
 
 FLOPS = 2 * BATCH * K1 * HIDDEN + 2 * BATCH * HIDDEN * N_OUT
 
@@ -92,6 +97,11 @@ def tile_channel_net_pa_k_kernel(tc, x, noise, h, W1, b1, W2, b2, out):
         minus_h1 = const.tile([P, 1], F32)
         nc.gpsimd.tensor_scalar(
             out=minus_h1[:], in0=h_raw[:, 1:2], scalar1=-1.0, scalar2=0.0, op0=ALU.mult, op1=ALU.add
+        )
+
+        b2_planes = const.tile([P, N_OUT], F32)
+        nc.gpsimd.tensor_copy(
+            out=b2_planes[:].rearrange("p (c j) -> p c j", c=2), in_=b2_all[:].rearrange("p (j c) -> p c j", c=2)
         )
 
         acc = [acc_pool.tile([P, BATCH], F32, name="acc%d" % t) for t in range(PACK)]
@@ -163,8 +173,8 @@ def tile_channel_net_pa_k_kernel(tc, x, noise, h, W1, b1, W2, b2, out):
                 nc.tensor.transpose(w2_flipped[:, u, :], w2_words[:, u, :], ident[:])
             w2_grouped = const.tile([P, N_OUT * PACK], BF16, align_bytes=64)
             nc.scalar.copy(
-                out=w2_grouped[:].bitcast(F32).rearrange("p (n u) -> p n u", u=HALVES),
-                in_=w2_flipped[:].rearrange("p u n -> p n u"),
+                out=w2_grouped[:].bitcast(F32).rearrange("p (c j u) -> p c j u", c=2, u=HALVES),
+                in_=w2_flipped[:].rearrange("p u (j c) -> p c j u", c=2),
             )
             w2_codes = const.tile([P, N_OUT], U32, align_bytes=64)
             w2_scales = const.tile([P, N_OUT], U8, align_bytes=64)
@@ -198,30 +208,46 @@ def tile_channel_net_pa_k_kernel(tc, x, noise, h, W1, b1, W2, b2, out):
                     op0=ALU.add, op1=ALU.max,
                 )
         a_grouped = tail.tile([P, BATCH, PACK], BF16, align_bytes=64)
-        nc.vector.tensor_copy(out=a_grouped[:], in_=a_planes[:].rearrange("p t b -> p b t"))
+
+        def group_columns(copy, first, last):
+            copy(out=a_grouped[:, first:last, :], in_=a_planes[:, :, first:last].rearrange("p t b -> p b t"))
+
+        group_columns(nc.vector.tensor_copy, 0, SIDE_ROWS)
+        group_columns(nc.vector.tensor_copy, SIDE_ROWS, SIDE_ROWS + P)
+        group_columns(nc.scalar.copy, SIDE_ROWS + P, BATCH)
+
         a_codes = tail.tile([P, BATCH], U32, align_bytes=64)
         a_scales = tail.tile([P, BATCH], U8, align_bytes=64)
-        nc.vector.quantize_mx(
-            out=a_codes[:].bitcast(FP8X4), scales=a_scales[:], in_=a_grouped[:].rearrange("p b t -> p (b t)")
-        )
-
-        z_ps = bank_pool.tile([P, ROW_TILES, N_OUT], F32, tag="bank")
-        for t in range(ROW_TILES):
-            rows = slice(t * P, (t + 1) * P)
-            nc.tensor.matmul_mx(
-                out=z_ps[:, t, :],
-                lhsT=a_codes[:, rows].bitcast(FP8X4),
-                lhsT_scale=a_scales[:, rows],
-                rhs=w2_codes[:].bitcast(FP8X4),
-                rhs_scale=w2_scales[:],
-                start=True,
-                stop=True,
+        a_flat = a_grouped[:].rearrange("p b t -> p (b t)")
+        z = tail.tile([P, ROW_TILES, N_OUT], F32)
+        for side in range(SIDES):
+            cols = slice(side * SIDE_ROWS, (side + 1) * SIDE_ROWS)
+            nc.vector.quantize_mx(
+                out=a_codes[:, cols].bitcast(FP8X4),
+                scales=a_scales[:, cols],
+                in_=a_flat[:, side * SIDE_ROWS * PACK : (side + 1) * SIDE_ROWS * PACK],
+            )
+        for side in range(SIDES):
+            z_ps = bank_pool.tile([P, SIDE_TILES, N_OUT], F32, tag="bank")
+            for local in range(SIDE_TILES):
+                t = side * SIDE_TILES + local
+                rows = slice(t * P, (t + 1) * P)
+                nc.tensor.matmul_mx(
+                    out=z_ps[:, local, :],
+                    lhsT=a_codes[:, rows].bitcast(FP8X4),
+                    lhsT_scale=a_scales[:, rows],
+                    rhs=w2_codes[:].bitcast(FP8X4),
+                    rhs_scale=w2_scales[:],
+                    start=True,
+                    stop=True,
+                )
+            nc.vector.tensor_tensor(
+                out=z[:, side * SIDE_TILES : (side + 1) * SIDE_TILES, :],
+                in0=z_ps[:],
+                in1=b2_planes[:].unsqueeze(1).to_broadcast([P, SIDE_TILES, N_OUT]),
+                op=ALU.add,
             )
 
-        z = tail.tile([P, ROW_TILES, N_OUT], F32)
-        nc.vector.tensor_tensor(
-            out=z[:], in0=z_ps[:], in1=b2_all[:].unsqueeze(1).to_broadcast([P, ROW_TILES, N_OUT]), op=ALU.add
-        )
         squares = tail.tile([P, ROW_TILES, N_OUT], F32)
         sum_sq = tail.tile([P, ROW_TILES], F32)
         for t in range(ROW_TILES):
@@ -229,29 +255,36 @@ def tile_channel_net_pa_k_kernel(tc, x, noise, h, W1, b1, W2, b2, out):
                 out=squares[:, t, :], in_=z[:, t, :], func=ACT.Square, accum_out=sum_sq[:, t : t + 1]
             )
         norm_by_8 = tail.tile([P, ROW_TILES], F32)
-        nc.scalar.activation(out=norm_by_8[:], in_=sum_sq[:], func=ACT.Sqrt, scale=2.0 / N_OUT)
+        nc.scalar.activation(out=norm_by_8[:], in_=sum_sq[:], func=ACT.Sqrt, scale=1.0 / PAIRS)
 
         z_h0 = tail.tile([P, ROW_TILES, N_OUT], F32)
         turned = tail.tile([P, ROW_TILES, N_OUT], F32)
         nc.vector.tensor_scalar(out=z_h0[:], in0=z[:], scalar1=h_f[:, 0:1], scalar2=None, op0=ALU.mult)
-        z_pairs = z[:].rearrange("p t (j c) -> p (t j) c", c=2)
-        z_h0_pairs = z_h0[:].rearrange("p t (j c) -> p (t j) c", c=2)
-        turned_pairs = turned[:].rearrange("p t (j c) -> p (t j) c", c=2)
+        z_planes = z[:].rearrange("p t (c j) -> p t c j", c=2)
+        z_h0_planes = z_h0[:].rearrange("p t (c j) -> p t c j", c=2)
+        turned_planes = turned[:].rearrange("p t (c j) -> p t c j", c=2)
         nc.vector.scalar_tensor_tensor(
-            out=turned_pairs[:, :, 0], in0=z_pairs[:, :, 1], scalar=minus_h1[:, 0:1], in1=z_h0_pairs[:, :, 0],
-            op0=ALU.mult, op1=ALU.add,
+            out=turned_planes[:, :, 0, :], in0=z_planes[:, :, 1, :], scalar=minus_h1[:, 0:1],
+            in1=z_h0_planes[:, :, 0, :], op0=ALU.mult, op1=ALU.add,
         )
         nc.vector.scalar_tensor_tensor(
-            out=turned_pairs[:, :, 1], in0=z_pairs[:, :, 0], scalar=h_f[:, 1:2], in1=z_h0_pairs[:, :, 1],
-            op0=ALU.mult, op1=ALU.add,
+            out=turned_planes[:, :, 1, :], in0=z_planes[:, :, 0, :], scalar=h_f[:, 1:2],
+            in1=z_h0_planes[:, :, 1, :], op0=ALU.mult, op1=ALU.add,
         )
 
         gain = tail.tile([P, ROW_TILES], F32)
         nc.vector.reciprocal(out=gain[:], in_=norm_by_8[:])
         y = tail.tile([P, ROW_TILES, N_OUT], F32)
-        for t in range(ROW_TILES):
-            nc.vector.scalar_tensor_tensor(
-                out=y[:, t, :], in0=turned[:, t, :], scalar=gain[:, t : t + 1], in1=noise_sb[:, t, :],
-                op0=ALU.mult, op1=ALU.add,
-            )
-        nc.sync.dma_start(out=out.rearrange("(p t) n -> p t n", t=ROW_TILES), in_=y[:])
+        out_rows = out.rearrange("(p t) n -> p t n", t=ROW_TILES)
+        for side in range(SIDES):
+            tiles = slice(side * SIDE_TILES, (side + 1) * SIDE_TILES)
+            for t in range(side * SIDE_TILES, (side + 1) * SIDE_TILES):
+                nc.vector.scalar_tensor_tensor(
+                    out=y[:, t, :].rearrange("p (j c) -> p j c", c=2),
+                    in0=turned_planes[:, t, :, :].rearrange("p c j -> p j c"),
+                    scalar=gain[:, t : t + 1],
+                    in1=noise_sb[:, t, :].rearrange("p (j c) -> p j c", c=2),
+                    op0=ALU.mult,
+                    op1=ALU.add,
+                )
+            nc.sync.dma_start(out=out_rows[:, tiles, :], in_=y[:, tiles, :])

@@ -22,12 +22,14 @@ PASSES = K1 // K_PASS
 BANK_ROWS = 2 * P
 
 CHUNK_PASSES = 2
-CHUNK_K = CHUNK_PASSES * K_PASS
-CHUNKS = PASSES // CHUNK_PASSES
+HEAD_CHUNKS = 8
+CHUNK_STARTS = list(range(HEAD_CHUNKS)) + list(range(HEAD_CHUNKS, PASSES, CHUNK_PASSES))
+CHUNKS = len(CHUNK_STARTS)
 RAW_BUFS = 8
 
-PASSES_PER_ROUND = 1
-ROUNDS = PASSES // PASSES_PER_ROUND
+ROUND_STARTS = [0, 1, 2] + list(range(3, PASSES, 2))
+ROUND_PASSES = [range(a, b) for a, b in zip(ROUND_STARTS, ROUND_STARTS[1:] + [PASSES])]
+MOST_PASSES = max(len(passes) for passes in ROUND_PASSES)
 
 PAIRS = N_OUT // 2
 SIDES = 2
@@ -37,21 +39,13 @@ SIDE_ROWS = SIDE_TILES * P
 FLOPS = 2 * BATCH * K1 * HIDDEN + 2 * BATCH * HIDDEN * N_OUT
 
 
-def doubling_pieces(total, first):
-    cuts = [(0, first)]
-    while cuts[-1][1] < total:
-        end = cuts[-1][1]
-        cuts.append((end, 2 * end))
-    return cuts
-
-
 def tile_channel_net_pa_k_kernel(tc, x, noise, h, W1, b1, W2, b2, out):
     nc = tc.nc
     with ExitStack() as ctx:
         ctx.enter_context(tc.manual_schedule())
         const = ctx.enter_context(tc.tile_pool(name="const", bufs=1))
         raw_pool = ctx.enter_context(tc.tile_pool(name="raw", bufs=RAW_BUFS))
-        stage = ctx.enter_context(tc.tile_pool(name="stage", bufs=2 * PASSES_PER_ROUND))
+        stage = ctx.enter_context(tc.tile_pool(name="stage", bufs=2 * MOST_PASSES))
         tail = ctx.enter_context(tc.tile_pool(name="tail", bufs=1))
         acc_pool = ctx.enter_context(tc.psum_pool(name="acc", bufs=1))
         bank_pool = ctx.enter_context(tc.psum_pool(name="bank", bufs=4))
@@ -60,18 +54,21 @@ def tile_channel_net_pa_k_kernel(tc, x, noise, h, W1, b1, W2, b2, out):
         w1_rows = W1.rearrange("(p t) k -> p t k", t=ROW_TILES)
 
         def load_chunk(c):
-            x_raw = raw_pool.tile([P, ROW_TILES, CHUNK_K], BF16)
-            w_raw = raw_pool.tile([P, ROW_TILES, CHUNK_K], BF16)
-            pieces = doubling_pieces(CHUNK_K, K_PASS) if c == 0 else [(0, CHUNK_K)]
-            for lo, hi in pieces:
-                k_range = slice(c * CHUNK_K + lo, c * CHUNK_K + hi)
-                nc.sync.dma_start(out=x_raw[:, :, lo:hi], in_=x_rows[:, :, k_range])
-                nc.sync.dma_start(out=w_raw[:, :, lo:hi], in_=w1_rows[:, :, k_range])
-            return x_raw, w_raw
+            first = CHUNK_STARTS[c]
+            count = 1 if c < HEAD_CHUNKS else CHUNK_PASSES
+            k_range = slice(first * K_PASS, (first + count) * K_PASS)
+            x_raw = raw_pool.tile([P, ROW_TILES, count * K_PASS], BF16)
+            w_raw = raw_pool.tile([P, ROW_TILES, count * K_PASS], BF16)
+            rows_step = ROW_TILES // 2 if c == 0 else ROW_TILES
+            for raw, rows in ((x_raw, x_rows), (w_raw, w1_rows)):
+                for t in range(0, ROW_TILES, rows_step):
+                    nc.sync.dma_start(out=raw[:, t : t + rows_step, :], in_=rows[:, t : t + rows_step, k_range])
+            for g in range(first, first + count):
+                raw_of[g] = (x_raw, w_raw, g - first, c if g == first + count - 1 else None)
 
-        chunks = {}
+        raw_of = {}
         for c in range(RAW_BUFS):
-            chunks[c] = load_chunk(c)
+            load_chunk(c)
 
         w2_raw = const.tile([P, HIDDEN], BF16)
         nc.sync.dma_start(out=w2_raw[:], in_=W2)
@@ -128,16 +125,15 @@ def tile_channel_net_pa_k_kernel(tc, x, noise, h, W1, b1, W2, b2, out):
         grouped_of = {}
         packed_of = {}
 
-        def flip(g):
-            c, g_in_chunk = divmod(g, CHUNK_PASSES)
-            x_raw, w_raw = chunks[c]
+        def flip(g, empty_x, empty_w):
+            x_raw, w_raw, g_in_chunk, last_of = raw_of[g]
             x_grouped = stage.tile([P, BATCH * PACK], BF16, align_bytes=64)
             w_grouped = stage.tile([P, HIDDEN * PACK], BF16, align_bytes=64)
-            k_onto_partitions(x_raw, g_in_chunk, x_grouped, [nc.vector.tensor_copy, nc.scalar.copy])
-            k_onto_partitions(w_raw, g_in_chunk, w_grouped, [nc.scalar.copy, nc.scalar.copy])
+            k_onto_partitions(x_raw, g_in_chunk, x_grouped, empty_x)
+            k_onto_partitions(w_raw, g_in_chunk, w_grouped, empty_w)
             grouped_of[g] = (x_grouped, w_grouped)
-            if g_in_chunk == CHUNK_PASSES - 1 and c + RAW_BUFS < CHUNKS:
-                chunks[c + RAW_BUFS] = load_chunk(c + RAW_BUFS)
+            if last_of is not None and last_of + RAW_BUFS < CHUNKS:
+                load_chunk(last_of + RAW_BUFS)
 
         def quantise(g):
             x_grouped, w_grouped = grouped_of[g]
@@ -163,10 +159,15 @@ def tile_channel_net_pa_k_kernel(tc, x, noise, h, W1, b1, W2, b2, out):
                     stop=(g == PASSES - 1),
                 )
 
-        def passes_of(rnd):
-            return range(rnd * PASSES_PER_ROUND, (rnd + 1) * PASSES_PER_ROUND)
+        def flip_round(passes):
+            vector, scalar = nc.vector.tensor_copy, nc.scalar.copy
+            if len(passes) == 1:
+                flip(passes[0], [vector, scalar], [scalar, scalar])
+            else:
+                flip(passes[0], [scalar, vector], [scalar, vector])
+                flip(passes[1], [scalar, vector], [scalar, scalar])
 
-        def flip_and_quantise_w2():
+        def flip_w2():
             w2_words = w2_raw[:].bitcast(F32).rearrange("n (p u) -> n u p", u=HALVES)
             w2_flipped = bank_pool.tile([P, HALVES, N_OUT], F32, tag="bank")
             for u in range(HALVES):
@@ -176,37 +177,49 @@ def tile_channel_net_pa_k_kernel(tc, x, noise, h, W1, b1, W2, b2, out):
                 out=w2_grouped[:].bitcast(F32).rearrange("p (c j u) -> p c j u", c=2, u=HALVES),
                 in_=w2_flipped[:].rearrange("p u (j c) -> p c j u", c=2),
             )
+            return w2_grouped
+
+        def quantise_w2(w2_grouped):
             w2_codes = const.tile([P, N_OUT], U32, align_bytes=64)
             w2_scales = const.tile([P, N_OUT], U8, align_bytes=64)
             nc.vector.quantize_mx(out=w2_codes[:].bitcast(FP8X4), scales=w2_scales[:], in_=w2_grouped[:])
             return w2_codes, w2_scales
 
-        for g in passes_of(0):
-            flip(g)
-        for g in passes_of(0):
+        flip_round(ROUND_PASSES[0])
+        for g in ROUND_PASSES[0]:
             quantise(g)
-        for rnd in range(1, ROUNDS):
-            for g in passes_of(rnd):
-                flip(g)
-            for g in passes_of(rnd - 1):
+        for before, passes in zip(ROUND_PASSES, ROUND_PASSES[1:]):
+            flip_round(passes)
+            if passes[-1] == PASSES - 1:
+                w2_grouped = flip_w2()
+            for g in before:
                 multiply(g)
-            for g in passes_of(rnd):
+            for g in passes:
                 quantise(g)
-        w2_codes, w2_scales = flip_and_quantise_w2()
-        for g in passes_of(ROUNDS - 1):
+        w2_codes, w2_scales = quantise_w2(w2_grouped)
+        for g in ROUND_PASSES[-1]:
             multiply(g)
 
         a_planes = tail.tile([P, PACK, BATCH], BF16)
-        for t in range(PACK):
-            if t % 2 == 0:
-                nc.scalar.activation(
-                    out=a_planes[:, t, :], in_=acc[t][:], func=ACT.Relu, bias=b1_f[:, t : t + 1], scale=1.0
-                )
-            else:
-                nc.vector.tensor_scalar(
-                    out=a_planes[:, t, :], in0=acc[t][:], scalar1=b1_f[:, t : t + 1], scalar2=0.0,
-                    op0=ALU.add, op1=ALU.max,
-                )
+
+        def relu_on_vector(t, first, last):
+            nc.vector.tensor_scalar(
+                out=a_planes[:, t, first:last], in0=acc[t][:, first:last], scalar1=b1_f[:, t : t + 1], scalar2=0.0,
+                op0=ALU.add, op1=ALU.max,
+            )
+
+        def relu_on_scalar(t, first, last):
+            nc.scalar.activation(
+                out=a_planes[:, t, first:last], in_=acc[t][:, first:last], func=ACT.Relu,
+                bias=b1_f[:, t : t + 1], scale=1.0,
+            )
+
+        relu_on_scalar(0, 0, BATCH)
+        relu_on_vector(1, 0, BATCH)
+        relu_on_scalar(2, 0, BATCH)
+        relu_on_vector(3, 0, SIDE_ROWS)
+        relu_on_scalar(3, SIDE_ROWS, BATCH)
+
         a_grouped = tail.tile([P, BATCH, PACK], BF16, align_bytes=64)
 
         def group_columns(copy, first, last):

@@ -27,10 +27,6 @@ CHUNK_STARTS = list(range(HEAD_CHUNKS)) + list(range(HEAD_CHUNKS, PASSES, CHUNK_
 CHUNKS = len(CHUNK_STARTS)
 RAW_BUFS = 8
 
-ROUND_STARTS = [0, 1, 2] + list(range(3, PASSES, 2))
-ROUND_PASSES = [range(a, b) for a, b in zip(ROUND_STARTS, ROUND_STARTS[1:] + [PASSES])]
-MOST_PASSES = max(len(passes) for passes in ROUND_PASSES)
-
 PAIRS = N_OUT // 2
 SIDES = 2
 SIDE_TILES = ROW_TILES // SIDES
@@ -45,7 +41,7 @@ def tile_channel_net_pa_k_kernel(tc, x, noise, h, W1, b1, W2, b2, out):
         ctx.enter_context(tc.manual_schedule())
         const = ctx.enter_context(tc.tile_pool(name="const", bufs=1))
         raw_pool = ctx.enter_context(tc.tile_pool(name="raw", bufs=RAW_BUFS))
-        stage = ctx.enter_context(tc.tile_pool(name="stage", bufs=2 * MOST_PASSES))
+        stage = ctx.enter_context(tc.tile_pool(name="stage", bufs=2))
         tail = ctx.enter_context(tc.tile_pool(name="tail", bufs=1))
         acc_pool = ctx.enter_context(tc.psum_pool(name="acc", bufs=1))
         bank_pool = ctx.enter_context(tc.psum_pool(name="bank", bufs=4))
@@ -125,12 +121,12 @@ def tile_channel_net_pa_k_kernel(tc, x, noise, h, W1, b1, W2, b2, out):
         grouped_of = {}
         packed_of = {}
 
-        def flip(g, empty_x, empty_w):
+        def flip(g):
             x_raw, w_raw, g_in_chunk, last_of = raw_of[g]
             x_grouped = stage.tile([P, BATCH * PACK], BF16, align_bytes=64)
             w_grouped = stage.tile([P, HIDDEN * PACK], BF16, align_bytes=64)
-            k_onto_partitions(x_raw, g_in_chunk, x_grouped, empty_x)
-            k_onto_partitions(w_raw, g_in_chunk, w_grouped, empty_w)
+            k_onto_partitions(x_raw, g_in_chunk, x_grouped, [nc.vector.tensor_copy, nc.scalar.copy])
+            k_onto_partitions(w_raw, g_in_chunk, w_grouped, [nc.scalar.copy, nc.scalar.copy])
             grouped_of[g] = (x_grouped, w_grouped)
             if last_of is not None and last_of + RAW_BUFS < CHUNKS:
                 load_chunk(last_of + RAW_BUFS)
@@ -159,14 +155,6 @@ def tile_channel_net_pa_k_kernel(tc, x, noise, h, W1, b1, W2, b2, out):
                     stop=(g == PASSES - 1),
                 )
 
-        def flip_round(passes):
-            vector, scalar = nc.vector.tensor_copy, nc.scalar.copy
-            if len(passes) == 1:
-                flip(passes[0], [vector, scalar], [scalar, scalar])
-            else:
-                flip(passes[0], [scalar, vector], [scalar, vector])
-                flip(passes[1], [scalar, vector], [scalar, scalar])
-
         def flip_w2():
             w2_words = w2_raw[:].bitcast(F32).rearrange("n (p u) -> n u p", u=HALVES)
             w2_flipped = bank_pool.tile([P, HALVES, N_OUT], F32, tag="bank")
@@ -185,20 +173,16 @@ def tile_channel_net_pa_k_kernel(tc, x, noise, h, W1, b1, W2, b2, out):
             nc.vector.quantize_mx(out=w2_codes[:].bitcast(FP8X4), scales=w2_scales[:], in_=w2_grouped[:])
             return w2_codes, w2_scales
 
-        flip_round(ROUND_PASSES[0])
-        for g in ROUND_PASSES[0]:
-            quantise(g)
-        for before, passes in zip(ROUND_PASSES, ROUND_PASSES[1:]):
-            flip_round(passes)
-            if passes[-1] == PASSES - 1:
+        flip(0)
+        quantise(0)
+        for g in range(1, PASSES):
+            flip(g)
+            if g == PASSES - 1:
                 w2_grouped = flip_w2()
-            for g in before:
-                multiply(g)
-            for g in passes:
-                quantise(g)
+            multiply(g - 1)
+            quantise(g)
         w2_codes, w2_scales = quantise_w2(w2_grouped)
-        for g in ROUND_PASSES[-1]:
-            multiply(g)
+        multiply(PASSES - 1)
 
         a_planes = tail.tile([P, PACK, BATCH], BF16)
 

@@ -19,12 +19,13 @@ HALVES = 2
 BATCH, K1, HIDDEN, N_OUT = 512, 16384, 512, 128
 ROW_TILES = BATCH // P
 PASSES = K1 // K_PASS
-BANK_ROWS = 2 * P
+BANK_TILES = 2
+BANK_ROWS = BANK_TILES * P
+PASS_BANKS = 2 * ROW_TILES // BANK_TILES
 
 CHUNK_PASSES = 2
-HEAD_CHUNKS = 8
-CHUNK_STARTS = list(range(HEAD_CHUNKS)) + list(range(HEAD_CHUNKS, PASSES, CHUNK_PASSES))
-CHUNKS = len(CHUNK_STARTS)
+CHUNKS = PASSES // CHUNK_PASSES
+HEAD_CHUNKS = 3
 RAW_BUFS = 8
 
 PAIRS = N_OUT // 2
@@ -41,7 +42,7 @@ def tile_channel_net_pa_k_kernel(tc, x, noise, h, W1, b1, W2, b2, out):
         ctx.enter_context(tc.manual_schedule())
         const = ctx.enter_context(tc.tile_pool(name="const", bufs=1))
         raw_pool = ctx.enter_context(tc.tile_pool(name="raw", bufs=RAW_BUFS))
-        stage = ctx.enter_context(tc.tile_pool(name="stage", bufs=2))
+        stage = ctx.enter_context(tc.tile_pool(name="stage", bufs=4))
         tail = ctx.enter_context(tc.tile_pool(name="tail", bufs=1))
         acc_pool = ctx.enter_context(tc.psum_pool(name="acc", bufs=1))
         bank_pool = ctx.enter_context(tc.psum_pool(name="bank", bufs=4))
@@ -50,17 +51,14 @@ def tile_channel_net_pa_k_kernel(tc, x, noise, h, W1, b1, W2, b2, out):
         w1_rows = W1.rearrange("(p t) k -> p t k", t=ROW_TILES)
 
         def load_chunk(c):
-            first = CHUNK_STARTS[c]
-            count = 1 if c < HEAD_CHUNKS else CHUNK_PASSES
-            k_range = slice(first * K_PASS, (first + count) * K_PASS)
-            x_raw = raw_pool.tile([P, ROW_TILES, count * K_PASS], BF16)
-            w_raw = raw_pool.tile([P, ROW_TILES, count * K_PASS], BF16)
-            rows_step = ROW_TILES // 2 if c == 0 else ROW_TILES
+            k_range = slice(c * CHUNK_PASSES * K_PASS, (c + 1) * CHUNK_PASSES * K_PASS)
+            x_raw = raw_pool.tile([P, ROW_TILES, CHUNK_PASSES * K_PASS], BF16)
+            w_raw = raw_pool.tile([P, ROW_TILES, CHUNK_PASSES * K_PASS], BF16)
+            step = BANK_TILES if c < HEAD_CHUNKS else ROW_TILES
             for raw, rows in ((x_raw, x_rows), (w_raw, w1_rows)):
-                for t in range(0, ROW_TILES, rows_step):
-                    nc.sync.dma_start(out=raw[:, t : t + rows_step, :], in_=rows[:, t : t + rows_step, k_range])
-            for g in range(first, first + count):
-                raw_of[g] = (x_raw, w_raw, g - first, c if g == first + count - 1 else None)
+                for t in range(0, ROW_TILES, step):
+                    nc.sync.dma_start(out=raw[:, t : t + step, :], in_=rows[:, t : t + step, k_range])
+            raw_of[c] = (x_raw, w_raw)
 
         raw_of = {}
         for c in range(RAW_BUFS):
@@ -99,47 +97,46 @@ def tile_channel_net_pa_k_kernel(tc, x, noise, h, W1, b1, W2, b2, out):
 
         acc = [acc_pool.tile([P, BATCH], F32, name="acc%d" % t) for t in range(PACK)]
 
-        def k_onto_partitions(raw, g_in_chunk, grouped, copies):
-            words = raw[:].bitcast(F32)
-            grouped_words = grouped[:].bitcast(F32).rearrange("p (r u) -> p r u", u=HALVES)
-            first_word = g_in_chunk * (K_PASS // 2)
-            for bank in range(ROW_TILES * P // BANK_ROWS):
-                flipped = bank_pool.tile([P, HALVES, BANK_ROWS], F32, tag="bank")
-                for local in range(BANK_ROWS // P):
-                    row_tile = bank * (BANK_ROWS // P) + local
-                    for u in range(HALVES):
-                        nc.tensor.transpose(
-                            flipped[:, u, local * P : (local + 1) * P],
-                            words[:, row_tile, first_word + u * P : first_word + (u + 1) * P],
-                            ident[:],
-                        )
-                copies[bank](
-                    out=grouped_words[:, bank * BANK_ROWS : (bank + 1) * BANK_ROWS, :],
-                    in_=flipped[:].rearrange("p u r -> p r u"),
-                )
-
         grouped_of = {}
         packed_of = {}
 
-        def flip(g):
-            x_raw, w_raw, g_in_chunk, last_of = raw_of[g]
-            x_grouped = stage.tile([P, BATCH * PACK], BF16, align_bytes=64)
-            w_grouped = stage.tile([P, HIDDEN * PACK], BF16, align_bytes=64)
-            k_onto_partitions(x_raw, g_in_chunk, x_grouped, [nc.vector.tensor_copy, nc.scalar.copy])
-            k_onto_partitions(w_raw, g_in_chunk, w_grouped, [nc.scalar.copy, nc.scalar.copy])
-            grouped_of[g] = (x_grouped, w_grouped)
-            if last_of is not None and last_of + RAW_BUFS < CHUNKS:
-                load_chunk(last_of + RAW_BUFS)
+        def flip(g, bank):
+            c, g_in_chunk = divmod(g, CHUNK_PASSES)
+            operand, bank_of_operand = divmod(bank, PASS_BANKS // 2)
+            if bank == 0:
+                x_grouped = stage.tile([P, BATCH * PACK], BF16, align_bytes=64)
+                w_grouped = stage.tile([P, HIDDEN * PACK], BF16, align_bytes=64)
+                grouped_of[g] = (x_grouped, w_grouped)
+            words = raw_of[c][operand][:].bitcast(F32)
+            grouped_words = grouped_of[g][operand][:].bitcast(F32).rearrange("p (r u) -> p r u", u=HALVES)
+            first_word = g_in_chunk * (K_PASS // 2)
+            flipped = bank_pool.tile([P, HALVES, BANK_ROWS], F32, tag="bank")
+            for local in range(BANK_TILES):
+                for u in range(HALVES):
+                    nc.tensor.transpose(
+                        flipped[:, u, local * P : (local + 1) * P],
+                        words[:, bank_of_operand * BANK_TILES + local, first_word + u * P : first_word + (u + 1) * P],
+                        ident[:],
+                    )
+            copy = nc.vector.tensor_copy if bank == 0 else nc.scalar.copy
+            copy(
+                out=grouped_words[:, bank_of_operand * BANK_ROWS : (bank_of_operand + 1) * BANK_ROWS, :],
+                in_=flipped[:].rearrange("p u r -> p r u"),
+            )
+            if bank == PASS_BANKS - 1 and g_in_chunk == CHUNK_PASSES - 1 and c + RAW_BUFS < CHUNKS:
+                load_chunk(c + RAW_BUFS)
 
-        def quantise(g):
-            x_grouped, w_grouped = grouped_of[g]
+        def quantise_x(g):
             x_codes = stage.tile([P, BATCH], U32, align_bytes=64)
             x_scales = stage.tile([P, BATCH], U8, align_bytes=64)
+            nc.vector.quantize_mx(out=x_codes[:].bitcast(FP8X4), scales=x_scales[:], in_=grouped_of[g][0][:])
+            packed_of[g] = (x_codes, x_scales)
+
+        def quantise_w(g):
             w_codes = stage.tile([P, HIDDEN], U32, align_bytes=64)
             w_scales = stage.tile([P, HIDDEN], U8, align_bytes=64)
-            nc.vector.quantize_mx(out=x_codes[:].bitcast(FP8X4), scales=x_scales[:], in_=x_grouped[:])
-            nc.vector.quantize_mx(out=w_codes[:].bitcast(FP8X4), scales=w_scales[:], in_=w_grouped[:])
-            packed_of[g] = (x_codes, x_scales, w_codes, w_scales)
+            nc.vector.quantize_mx(out=w_codes[:].bitcast(FP8X4), scales=w_scales[:], in_=grouped_of[g][1][:])
+            packed_of[g] += (w_codes, w_scales)
 
         def multiply(g):
             x_codes, x_scales, w_codes, w_scales = packed_of[g]
@@ -173,15 +170,31 @@ def tile_channel_net_pa_k_kernel(tc, x, noise, h, W1, b1, W2, b2, out):
             nc.vector.quantize_mx(out=w2_codes[:].bitcast(FP8X4), scales=w2_scales[:], in_=w2_grouped[:])
             return w2_codes, w2_scales
 
-        flip(0)
-        quantise(0)
-        for g in range(1, PASSES):
-            flip(g)
+        for bank in range(PASS_BANKS):
+            flip(0, bank)
+            flip(1, bank)
+        for quantise in (quantise_x, quantise_w):
+            quantise(0)
+            quantise(1)
+        for bank in range(PASS_BANKS):
+            flip(2, bank)
+            flip(3, bank)
+            if bank == 1:
+                multiply(0)
+        multiply(1)
+        for quantise in (quantise_x, quantise_w):
+            quantise(2)
+            quantise(3)
+        for g in range(4, PASSES):
+            for bank in range(PASS_BANKS):
+                flip(g, bank)
             if g == PASSES - 1:
                 w2_grouped = flip_w2()
-            multiply(g - 1)
-            quantise(g)
+            multiply(g - 2)
+            quantise_x(g)
+            quantise_w(g)
         w2_codes, w2_scales = quantise_w2(w2_grouped)
+        multiply(PASSES - 2)
         multiply(PASSES - 1)
 
         a_planes = tail.tile([P, PACK, BATCH], BF16)

@@ -21,12 +21,16 @@ ROW_TILES = BATCH // P
 PASSES = K1 // K_PASS
 BANK_TILES = 2
 BANK_ROWS = BANK_TILES * P
-PASS_BANKS = 2 * ROW_TILES // BANK_TILES
+X_PIECES = ROW_TILES // BANK_TILES
 
 CHUNK_PASSES = 2
+CHUNK_K = CHUNK_PASSES * K_PASS
 CHUNKS = PASSES // CHUNK_PASSES
-HEAD_CHUNKS = 3
+HEAD_CHUNKS = 2
 RAW_BUFS = 8
+
+WARM_START, WARM_X, WARM_W = 4, 2, 1
+WARM_COLS = 512
 
 PAIRS = N_OUT // 2
 SIDES = 2
@@ -42,7 +46,7 @@ def tile_channel_net_pa_k_kernel(tc, x, noise, h, W1, b1, W2, b2, out):
         ctx.enter_context(tc.manual_schedule())
         const = ctx.enter_context(tc.tile_pool(name="const", bufs=1))
         raw_pool = ctx.enter_context(tc.tile_pool(name="raw", bufs=RAW_BUFS))
-        stage = ctx.enter_context(tc.tile_pool(name="stage", bufs=4))
+        stage = ctx.enter_context(tc.tile_pool(name="stage", bufs=2))
         tail = ctx.enter_context(tc.tile_pool(name="tail", bufs=1))
         acc_pool = ctx.enter_context(tc.psum_pool(name="acc", bufs=1))
         bank_pool = ctx.enter_context(tc.psum_pool(name="bank", bufs=4))
@@ -51,11 +55,11 @@ def tile_channel_net_pa_k_kernel(tc, x, noise, h, W1, b1, W2, b2, out):
         w1_rows = W1.rearrange("(p t) k -> p t k", t=ROW_TILES)
 
         def load_chunk(c):
-            k_range = slice(c * CHUNK_PASSES * K_PASS, (c + 1) * CHUNK_PASSES * K_PASS)
-            x_raw = raw_pool.tile([P, ROW_TILES, CHUNK_PASSES * K_PASS], BF16)
-            w_raw = raw_pool.tile([P, ROW_TILES, CHUNK_PASSES * K_PASS], BF16)
-            step = BANK_TILES if c < HEAD_CHUNKS else ROW_TILES
-            for raw, rows in ((x_raw, x_rows), (w_raw, w1_rows)):
+            k_range = slice(c * CHUNK_K, (c + 1) * CHUNK_K)
+            x_raw = raw_pool.tile([P, ROW_TILES, CHUNK_K], BF16)
+            w_raw = raw_pool.tile([P, ROW_TILES, CHUNK_K], BF16)
+            x_step, w_step = (BANK_TILES, 1) if c < HEAD_CHUNKS else (ROW_TILES, ROW_TILES)
+            for raw, rows, step in ((x_raw, x_rows, x_step), (w_raw, w1_rows, w_step)):
                 for t in range(0, ROW_TILES, step):
                     nc.sync.dma_start(out=raw[:, t : t + step, :], in_=rows[:, t : t + step, k_range])
             raw_of[c] = (x_raw, w_raw)
@@ -75,6 +79,8 @@ def tile_channel_net_pa_k_kernel(tc, x, noise, h, W1, b1, W2, b2, out):
         noise_sb = const.tile([P, ROW_TILES, N_OUT], BF16)
         nc.sync.dma_start(out=noise_sb[:], in_=noise.rearrange("(p t) n -> p t n", t=ROW_TILES))
 
+        zeros = const.tile([P, WARM_COLS], BF16)
+        nc.vector.memset(zeros[:], 0.0)
         one = const.tile([P, 1], F32)
         nc.vector.memset(one[:], 1.0)
         nc.scalar.activation(out=one[:], in_=one[:], func=ACT.Sqrt)
@@ -97,60 +103,86 @@ def tile_channel_net_pa_k_kernel(tc, x, noise, h, W1, b1, W2, b2, out):
 
         acc = [acc_pool.tile([P, BATCH], F32, name="acc%d" % t) for t in range(PACK)]
 
-        grouped_of = {}
-        packed_of = {}
+        def transpose_words(out, raw, row_tile, first_word):
+            words = raw[:].bitcast(F32)[:, row_tile, first_word : first_word + P]
+            nc.tensor.transpose(out, words, ident[:])
 
-        def flip(g, bank):
-            c, g_in_chunk = divmod(g, CHUNK_PASSES)
-            operand, bank_of_operand = divmod(bank, PASS_BANKS // 2)
-            if bank == 0:
-                x_grouped = stage.tile([P, BATCH * PACK], BF16, align_bytes=64)
-                w_grouped = stage.tile([P, HIDDEN * PACK], BF16, align_bytes=64)
-                grouped_of[g] = (x_grouped, w_grouped)
-            words = raw_of[c][operand][:].bitcast(F32)
-            grouped_words = grouped_of[g][operand][:].bitcast(F32).rearrange("p (r u) -> p r u", u=HALVES)
-            first_word = g_in_chunk * (K_PASS // 2)
-            flipped = bank_pool.tile([P, HALVES, BANK_ROWS], F32, tag="bank")
-            for local in range(BANK_TILES):
+        def empty_bank(first, out, in_):
+            copy = nc.vector.tensor_copy if first else nc.scalar.copy
+            copy(out=out, in_=in_)
+
+        x_grouped_of, x_packed_of, w_grouped_of, w_packed_of = {}, {}, {}, {}
+
+        def flip_x(c, piece):
+            for g in range(CHUNK_PASSES):
+                if piece == 0:
+                    x_grouped = stage.tile([P, BATCH * PACK], BF16, bufs=4, align_bytes=64)
+                    x_grouped_of[c, g] = x_grouped
+                flipped = bank_pool.tile([P, HALVES, BANK_ROWS], F32, tag="bank")
+                for local in range(BANK_TILES):
+                    for u in range(HALVES):
+                        transpose_words(
+                            flipped[:, u, local * P : (local + 1) * P],
+                            raw_of[c][0], piece * BANK_TILES + local, (g * HALVES + u) * P,
+                        )
+                grouped_words = x_grouped_of[c, g][:].bitcast(F32).rearrange("p (r u) -> p r u", u=HALVES)
+                empty_bank(
+                    piece == 0 and g == 0,
+                    grouped_words[:, piece * BANK_ROWS : (piece + 1) * BANK_ROWS, :],
+                    flipped[:].rearrange("p u r -> p r u"),
+                )
+
+        def quantise_x(c):
+            for g in range(CHUNK_PASSES):
+                x_codes = stage.tile([P, BATCH], U32, bufs=4, align_bytes=64)
+                x_scales = stage.tile([P, BATCH], U8, bufs=4, align_bytes=64)
+                nc.vector.quantize_mx(out=x_codes[:].bitcast(FP8X4), scales=x_scales[:], in_=x_grouped_of[c, g][:])
+                x_packed_of[c, g] = (x_codes, x_scales)
+
+        def flip_w(c, t):
+            if t == 0:
+                w_grouped = stage.tile([P, ROW_TILES, CHUNK_PASSES * P * PACK], BF16, bufs=2, align_bytes=64)
+                w_grouped_of[c] = w_grouped
+            flipped = bank_pool.tile([P, CHUNK_PASSES, HALVES, P], F32, tag="bank")
+            for g in range(CHUNK_PASSES):
                 for u in range(HALVES):
-                    nc.tensor.transpose(
-                        flipped[:, u, local * P : (local + 1) * P],
-                        words[:, bank_of_operand * BANK_TILES + local, first_word + u * P : first_word + (u + 1) * P],
-                        ident[:],
-                    )
-            copy = nc.vector.tensor_copy if bank == 0 else nc.scalar.copy
-            copy(
-                out=grouped_words[:, bank_of_operand * BANK_ROWS : (bank_of_operand + 1) * BANK_ROWS, :],
-                in_=flipped[:].rearrange("p u r -> p r u"),
+                    transpose_words(flipped[:, g, u, :], raw_of[c][1], t, (g * HALVES + u) * P)
+            empty_bank(
+                t == 0,
+                w_grouped_of[c][:, t, :].bitcast(F32).rearrange("p (g r u) -> p g r u", g=CHUNK_PASSES, u=HALVES),
+                flipped[:].rearrange("p g u r -> p g r u"),
             )
-            if bank == PASS_BANKS - 1 and g_in_chunk == CHUNK_PASSES - 1 and c + RAW_BUFS < CHUNKS:
+            if t == ROW_TILES - 1 and c + RAW_BUFS < CHUNKS:
                 load_chunk(c + RAW_BUFS)
 
-        def quantise_x(g):
-            x_codes = stage.tile([P, BATCH], U32, align_bytes=64)
-            x_scales = stage.tile([P, BATCH], U8, align_bytes=64)
-            nc.vector.quantize_mx(out=x_codes[:].bitcast(FP8X4), scales=x_scales[:], in_=grouped_of[g][0][:])
-            packed_of[g] = (x_codes, x_scales)
-
-        def quantise_w(g):
-            w_codes = stage.tile([P, HIDDEN], U32, align_bytes=64)
-            w_scales = stage.tile([P, HIDDEN], U8, align_bytes=64)
-            nc.vector.quantize_mx(out=w_codes[:].bitcast(FP8X4), scales=w_scales[:], in_=grouped_of[g][1][:])
-            packed_of[g] += (w_codes, w_scales)
-
-        def multiply(g):
-            x_codes, x_scales, w_codes, w_scales = packed_of[g]
-            for t in range(PACK):
-                units = slice(t * P, (t + 1) * P)
-                nc.tensor.matmul_mx(
-                    out=acc[t][:],
-                    lhsT=w_codes[:, units].bitcast(FP8X4),
-                    lhsT_scale=w_scales[:, units],
-                    rhs=x_codes[:].bitcast(FP8X4),
-                    rhs_scale=x_scales[:],
-                    start=(g == 0),
-                    stop=(g == PASSES - 1),
+        def quantise_w(c):
+            w_codes = stage.tile([P, ROW_TILES, CHUNK_PASSES * P], U32, bufs=2, align_bytes=64)
+            w_scales = stage.tile([P, ROW_TILES, CHUNK_PASSES * P], U8, bufs=2, align_bytes=64)
+            for t in range(ROW_TILES):
+                nc.vector.quantize_mx(
+                    out=w_codes[:, t, :].bitcast(FP8X4), scales=w_scales[:, t, :], in_=w_grouped_of[c][:, t, :]
                 )
+            w_packed_of[c] = (w_codes, w_scales)
+
+        def multiply(c, tiles):
+            w_codes, w_scales = w_packed_of[c]
+            for t in tiles:
+                for g in range(CHUNK_PASSES):
+                    x_codes, x_scales = x_packed_of[c, g]
+                    units = slice(g * P, (g + 1) * P)
+                    nc.tensor.matmul_mx(
+                        out=acc[t][:],
+                        lhsT=w_codes[:, t, units].bitcast(FP8X4),
+                        lhsT_scale=w_scales[:, t, units],
+                        rhs=x_codes[:].bitcast(FP8X4),
+                        rhs_scale=x_scales[:],
+                        start=(c == 0 and g == 0),
+                        stop=(c == CHUNKS - 1 and g == CHUNK_PASSES - 1),
+                    )
+
+        def keep_warm(count):
+            for i in range(count):
+                nc.tensor.matmul(acc[0][:], lhsT=zeros[:, :P], rhs=zeros[:], start=True, stop=True)
 
         def flip_w2():
             w2_words = w2_raw[:].bitcast(F32).rearrange("n (p u) -> n u p", u=HALVES)
@@ -170,32 +202,26 @@ def tile_channel_net_pa_k_kernel(tc, x, noise, h, W1, b1, W2, b2, out):
             nc.vector.quantize_mx(out=w2_codes[:].bitcast(FP8X4), scales=w2_scales[:], in_=w2_grouped[:])
             return w2_codes, w2_scales
 
-        for bank in range(PASS_BANKS):
-            flip(0, bank)
-            flip(1, bank)
-        for quantise in (quantise_x, quantise_w):
-            quantise(0)
-            quantise(1)
-        for bank in range(PASS_BANKS):
-            flip(2, bank)
-            flip(3, bank)
-            if bank == 1:
-                multiply(0)
-        multiply(1)
-        for quantise in (quantise_x, quantise_w):
-            quantise(2)
-            quantise(3)
-        for g in range(4, PASSES):
-            for bank in range(PASS_BANKS):
-                flip(g, bank)
-            if g == PASSES - 1:
+        keep_warm(WARM_START)
+        for c in range(CHUNKS):
+            for piece in range(X_PIECES):
+                flip_x(c, piece)
+                if c == 0:
+                    keep_warm(WARM_X)
+            if c > 0:
+                multiply(c - 1, [0, 1])
+            quantise_x(c)
+            for t in range(ROW_TILES):
+                flip_w(c, t)
+                if c == 0:
+                    keep_warm(WARM_W)
+            if c == CHUNKS - 1:
                 w2_grouped = flip_w2()
-            multiply(g - 2)
-            quantise_x(g)
-            quantise_w(g)
+            if c > 0:
+                multiply(c - 1, [2, 3])
+            quantise_w(c)
         w2_codes, w2_scales = quantise_w2(w2_grouped)
-        multiply(PASSES - 2)
-        multiply(PASSES - 1)
+        multiply(CHUNKS - 1, range(ROW_TILES))
 
         a_planes = tail.tile([P, PACK, BATCH], BF16)
 

@@ -26,11 +26,13 @@ X_PIECES = ROW_TILES // BANK_TILES
 CHUNK_PASSES = 2
 CHUNK_K = CHUNK_PASSES * K_PASS
 CHUNKS = PASSES // CHUNK_PASSES
-HEAD_CHUNKS = 2
+PIECED_CHUNKS = (0, 1, CHUNKS - 1)
 RAW_BUFS = 8
 
 WARM_START, WARM_X, WARM_W = 4, 2, 1
 WARM_COLS = 512
+
+SMALL_CHUNK = CHUNKS - 4
 
 PAIRS = N_OUT // 2
 SIDES = 2
@@ -58,7 +60,7 @@ def tile_channel_net_pa_k_kernel(tc, x, noise, h, W1, b1, W2, b2, out):
             k_range = slice(c * CHUNK_K, (c + 1) * CHUNK_K)
             x_raw = raw_pool.tile([P, ROW_TILES, CHUNK_K], BF16)
             w_raw = raw_pool.tile([P, ROW_TILES, CHUNK_K], BF16)
-            x_step, w_step = (BANK_TILES, 1) if c < HEAD_CHUNKS else (ROW_TILES, ROW_TILES)
+            x_step, w_step = (BANK_TILES, 1) if c in PIECED_CHUNKS else (ROW_TILES, ROW_TILES)
             for raw, rows, step in ((x_raw, x_rows, x_step), (w_raw, w1_rows, w_step)):
                 for t in range(0, ROW_TILES, step):
                     nc.sync.dma_start(out=raw[:, t : t + step, :], in_=rows[:, t : t + step, k_range])
@@ -68,14 +70,13 @@ def tile_channel_net_pa_k_kernel(tc, x, noise, h, W1, b1, W2, b2, out):
         for c in range(RAW_BUFS):
             load_chunk(c)
 
+        small = const.tile([P, HIDDEN + N_OUT + 2], BF16)
+        nc.gpsimd.memset(small[:], 0.0)
+        for first, vector in ((0, b1), (HIDDEN, b2), (HIDDEN + N_OUT, h)):
+            width = vector.shape[0]
+            nc.sync.dma_start(out=small[0:1, first : first + width], in_=vector.rearrange("(o n) -> o n", o=1))
         w2_raw = const.tile([P, HIDDEN], BF16)
         nc.sync.dma_start(out=w2_raw[:], in_=W2)
-        b1_raw = const.tile([P, PACK], BF16)
-        nc.sync.dma_start(out=b1_raw[:], in_=b1.rearrange("(p t) -> p t", t=PACK))
-        h_raw = const.tile([P, 2], BF16)
-        nc.sync.dma_start(out=h_raw[:], in_=h.partition_broadcast(P))
-        b2_all = const.tile([P, N_OUT], BF16)
-        nc.sync.dma_start(out=b2_all[:], in_=b2.partition_broadcast(P))
         noise_sb = const.tile([P, ROW_TILES, N_OUT], BF16)
         nc.sync.dma_start(out=noise_sb[:], in_=noise.rearrange("(p t) n -> p t n", t=ROW_TILES))
 
@@ -87,19 +88,27 @@ def tile_channel_net_pa_k_kernel(tc, x, noise, h, W1, b1, W2, b2, out):
 
         ident = const.tile([P, P], F32)
         make_identity(nc, ident[:])
+        ones = const.tile([P, P], BF16)
+        nc.vector.memset(ones[:], 1.0)
         b1_f = const.tile([P, PACK], F32)
-        nc.gpsimd.tensor_copy(out=b1_f[:], in_=b1_raw[:])
-        h_f = const.tile([P, 2], F32)
-        nc.gpsimd.tensor_copy(out=h_f[:], in_=h_raw[:])
-        minus_h1 = const.tile([P, 1], F32)
-        nc.gpsimd.tensor_scalar(
-            out=minus_h1[:], in0=h_raw[:, 1:2], scalar1=-1.0, scalar2=0.0, op0=ALU.mult, op1=ALU.add
-        )
-
         b2_planes = const.tile([P, N_OUT], F32)
-        nc.gpsimd.tensor_copy(
-            out=b2_planes[:].rearrange("p (c j) -> p c j", c=2), in_=b2_all[:].rearrange("p (j c) -> p c j", c=2)
-        )
+        h_f = const.tile([P, 2], F32)
+        minus_h1 = const.tile([P, 1], F32)
+
+        def spread_small_vectors():
+            spread = bank_pool.tile([P, PACK + N_OUT + 2], F32, tag="bank")
+            for t in range(PACK):
+                nc.tensor.matmul(
+                    spread[:, t : t + 1], lhsT=small[:, t:HIDDEN:PACK], rhs=ones[:, 0:1], start=True, stop=True
+                )
+            nc.tensor.matmul(spread[:, PACK:], lhsT=ones[:], rhs=small[:, HIDDEN:], start=True, stop=True)
+            nc.scalar.copy(out=b1_f[:], in_=spread[:, :PACK])
+            nc.scalar.copy(
+                out=b2_planes[:].rearrange("p (c j) -> p c j", c=2),
+                in_=spread[:, PACK : PACK + N_OUT].rearrange("p (j c) -> p c j", c=2),
+            )
+            nc.scalar.copy(out=h_f[:], in_=spread[:, PACK + N_OUT :])
+            nc.scalar.mul(minus_h1[:], spread[:, PACK + N_OUT + 1 :], -1.0)
 
         acc = [acc_pool.tile([P, BATCH], F32, name="acc%d" % t) for t in range(PACK)]
 
@@ -139,7 +148,7 @@ def tile_channel_net_pa_k_kernel(tc, x, noise, h, W1, b1, W2, b2, out):
                 nc.vector.quantize_mx(out=x_codes[:].bitcast(FP8X4), scales=x_scales[:], in_=x_grouped_of[c, g][:])
                 x_packed_of[c, g] = (x_codes, x_scales)
 
-        def flip_w(c, t):
+        def flip_w(c, t, on_vector):
             if t == 0:
                 w_grouped = stage.tile([P, ROW_TILES, CHUNK_PASSES * P * PACK], BF16, bufs=2, align_bytes=64)
                 w_grouped_of[c] = w_grouped
@@ -148,21 +157,23 @@ def tile_channel_net_pa_k_kernel(tc, x, noise, h, W1, b1, W2, b2, out):
                 for u in range(HALVES):
                     transpose_words(flipped[:, g, u, :], raw_of[c][1], t, (g * HALVES + u) * P)
             empty_bank(
-                t == 0,
+                on_vector,
                 w_grouped_of[c][:, t, :].bitcast(F32).rearrange("p (g r u) -> p g r u", g=CHUNK_PASSES, u=HALVES),
                 flipped[:].rearrange("p g u r -> p g r u"),
             )
             if t == ROW_TILES - 1 and c + RAW_BUFS < CHUNKS:
                 load_chunk(c + RAW_BUFS)
 
-        def quantise_w(c):
-            w_codes = stage.tile([P, ROW_TILES, CHUNK_PASSES * P], U32, bufs=2, align_bytes=64)
-            w_scales = stage.tile([P, ROW_TILES, CHUNK_PASSES * P], U8, bufs=2, align_bytes=64)
-            for t in range(ROW_TILES):
+        def quantise_w(c, tiles):
+            if tiles[0] == 0:
+                w_codes = stage.tile([P, ROW_TILES, CHUNK_PASSES * P], U32, bufs=2, align_bytes=64)
+                w_scales = stage.tile([P, ROW_TILES, CHUNK_PASSES * P], U8, bufs=2, align_bytes=64)
+                w_packed_of[c] = (w_codes, w_scales)
+            w_codes, w_scales = w_packed_of[c]
+            for t in tiles:
                 nc.vector.quantize_mx(
                     out=w_codes[:, t, :].bitcast(FP8X4), scales=w_scales[:, t, :], in_=w_grouped_of[c][:, t, :]
                 )
-            w_packed_of[c] = (w_codes, w_scales)
 
         def multiply(c, tiles):
             w_codes, w_scales = w_packed_of[c]
@@ -203,7 +214,7 @@ def tile_channel_net_pa_k_kernel(tc, x, noise, h, W1, b1, W2, b2, out):
             return w2_codes, w2_scales
 
         keep_warm(WARM_START)
-        for c in range(CHUNKS):
+        for c in range(CHUNKS - 1):
             for piece in range(X_PIECES):
                 flip_x(c, piece)
                 if c == 0:
@@ -212,16 +223,27 @@ def tile_channel_net_pa_k_kernel(tc, x, noise, h, W1, b1, W2, b2, out):
                 multiply(c - 1, [0, 1])
             quantise_x(c)
             for t in range(ROW_TILES):
-                flip_w(c, t)
+                flip_w(c, t, t == 0)
                 if c == 0:
                     keep_warm(WARM_W)
-            if c == CHUNKS - 1:
+            if c == SMALL_CHUNK:
                 w2_grouped = flip_w2()
+                spread_small_vectors()
             if c > 0:
                 multiply(c - 1, [2, 3])
-            quantise_w(c)
-        w2_codes, w2_scales = quantise_w2(w2_grouped)
-        multiply(CHUNKS - 1, range(ROW_TILES))
+            quantise_w(c, range(ROW_TILES))
+            if c == SMALL_CHUNK:
+                w2_codes, w2_scales = quantise_w2(w2_grouped)
+        last = CHUNKS - 1
+        for piece in range(X_PIECES):
+            flip_x(last, piece)
+        multiply(last - 1, [0, 1, 2])
+        quantise_x(last)
+        for t in range(ROW_TILES):
+            flip_w(last, t, False)
+            quantise_w(last, [t])
+        multiply(last - 1, [3])
+        multiply(last, range(ROW_TILES))
 
         a_planes = tail.tile([P, PACK, BATCH], BF16)
 

@@ -34,6 +34,12 @@ WARM_COLS = 512
 
 SMALL_CHUNK = CHUNKS - 4
 
+TILE_COLS = CHUNK_PASSES * P
+STAGGER = 256
+X_SCALES_START = 64
+W_CODES_START = 32
+W_SCALES_START = 192
+
 PAIRS = N_OUT // 2
 SIDES = 2
 SIDE_TILES = ROW_TILES // SIDES
@@ -143,10 +149,12 @@ def tile_channel_net_pa_k_kernel(tc, x, noise, h, W1, b1, W2, b2, out):
 
         def quantise_x(c):
             for g in range(CHUNK_PASSES):
-                x_codes = stage.tile([P, BATCH], U32, bufs=4, align_bytes=64)
-                x_scales = stage.tile([P, BATCH], U8, bufs=4, align_bytes=64)
-                nc.vector.quantize_mx(out=x_codes[:].bitcast(FP8X4), scales=x_scales[:], in_=x_grouped_of[c, g][:])
-                x_packed_of[c, g] = (x_codes, x_scales)
+                x_codes = stage.tile([P, BATCH], U32, bufs=4, align_bytes=STAGGER)
+                x_scales = stage.tile([P, X_SCALES_START + BATCH], U8, bufs=4, align_bytes=STAGGER)
+                x_packed_of[c, g] = (x_codes[:], x_scales[:, X_SCALES_START:])
+                nc.vector.quantize_mx(
+                    out=x_codes[:].bitcast(FP8X4), scales=x_scales[:, X_SCALES_START:], in_=x_grouped_of[c, g][:]
+                )
 
         def flip_w(c, t, on_vector):
             if t == 0:
@@ -166,13 +174,14 @@ def tile_channel_net_pa_k_kernel(tc, x, noise, h, W1, b1, W2, b2, out):
 
         def quantise_w(c, tiles):
             if tiles[0] == 0:
-                w_codes = stage.tile([P, ROW_TILES, CHUNK_PASSES * P], U32, bufs=2, align_bytes=64)
-                w_scales = stage.tile([P, ROW_TILES, CHUNK_PASSES * P], U8, bufs=2, align_bytes=64)
-                w_packed_of[c] = (w_codes, w_scales)
-            w_codes, w_scales = w_packed_of[c]
+                w_codes = stage.tile([P, W_CODES_START + TILE_COLS * ROW_TILES], U32, bufs=2, align_bytes=STAGGER)
+                w_scales = stage.tile([P, W_SCALES_START + TILE_COLS * ROW_TILES], U8, bufs=2, align_bytes=STAGGER)
+                w_packed_of[c] = (w_codes[:, W_CODES_START:], w_scales[:, W_SCALES_START:])
+            codes, scales = w_packed_of[c]
             for t in tiles:
+                cols = slice(t * TILE_COLS, (t + 1) * TILE_COLS)
                 nc.vector.quantize_mx(
-                    out=w_codes[:, t, :].bitcast(FP8X4), scales=w_scales[:, t, :], in_=w_grouped_of[c][:, t, :]
+                    out=codes[:, cols].bitcast(FP8X4), scales=scales[:, cols], in_=w_grouped_of[c][:, t, :]
                 )
 
         def multiply(c, tiles):
@@ -180,13 +189,13 @@ def tile_channel_net_pa_k_kernel(tc, x, noise, h, W1, b1, W2, b2, out):
             for t in tiles:
                 for g in range(CHUNK_PASSES):
                     x_codes, x_scales = x_packed_of[c, g]
-                    units = slice(g * P, (g + 1) * P)
+                    units = slice(t * TILE_COLS + g * P, t * TILE_COLS + (g + 1) * P)
                     nc.tensor.matmul_mx(
                         out=acc[t][:],
-                        lhsT=w_codes[:, t, units].bitcast(FP8X4),
-                        lhsT_scale=w_scales[:, t, units],
-                        rhs=x_codes[:].bitcast(FP8X4),
-                        rhs_scale=x_scales[:],
+                        lhsT=w_codes[:, units].bitcast(FP8X4),
+                        lhsT_scale=w_scales[:, units],
+                        rhs=x_codes.bitcast(FP8X4),
+                        rhs_scale=x_scales,
                         start=(c == 0 and g == 0),
                         stop=(c == CHUNKS - 1 and g == CHUNK_PASSES - 1),
                     )

@@ -39,6 +39,7 @@ STAGGER = 256
 X_SCALES_START = 64
 W_CODES_START = 32
 W_SCALES_START = 192
+IDENT_START = 32
 
 PAIRS = N_OUT // 2
 SIDES = 2
@@ -64,8 +65,8 @@ def tile_channel_net_pa_k_kernel(tc, x, noise, h, W1, b1, W2, b2, out):
 
         def load_chunk(c):
             k_range = slice(c * CHUNK_K, (c + 1) * CHUNK_K)
-            x_raw = raw_pool.tile([P, ROW_TILES, CHUNK_K], BF16)
-            w_raw = raw_pool.tile([P, ROW_TILES, CHUNK_K], BF16)
+            x_raw = raw_pool.tile([P, ROW_TILES, CHUNK_K], BF16, align_bytes=STAGGER)
+            w_raw = raw_pool.tile([P, ROW_TILES, CHUNK_K], BF16, align_bytes=STAGGER)
             x_step, w_step = (BANK_TILES, 1) if c in PIECED_CHUNKS else (ROW_TILES, ROW_TILES)
             for raw, rows, step in ((x_raw, x_rows, x_step), (w_raw, w1_rows, w_step)):
                 for t in range(0, ROW_TILES, step):
@@ -92,8 +93,9 @@ def tile_channel_net_pa_k_kernel(tc, x, noise, h, W1, b1, W2, b2, out):
         nc.vector.memset(one[:], 1.0)
         nc.scalar.activation(out=one[:], in_=one[:], func=ACT.Sqrt)
 
-        ident = const.tile([P, P], F32)
-        make_identity(nc, ident[:])
+        ident_tile = const.tile([P, IDENT_START + P], F32, align_bytes=STAGGER)
+        ident = ident_tile[:, IDENT_START:]
+        make_identity(nc, ident)
         ones = const.tile([P, P], BF16)
         nc.vector.memset(ones[:], 1.0)
         b1_f = const.tile([P, PACK], F32)
@@ -120,7 +122,7 @@ def tile_channel_net_pa_k_kernel(tc, x, noise, h, W1, b1, W2, b2, out):
 
         def transpose_words(out, raw, row_tile, first_word):
             words = raw[:].bitcast(F32)[:, row_tile, first_word : first_word + P]
-            nc.tensor.transpose(out, words, ident[:])
+            nc.tensor.transpose(out, words, ident)
 
         def empty_bank(first, out, in_):
             copy = nc.vector.tensor_copy if first else nc.scalar.copy
@@ -172,28 +174,35 @@ def tile_channel_net_pa_k_kernel(tc, x, noise, h, W1, b1, W2, b2, out):
             if t == ROW_TILES - 1 and c + RAW_BUFS < CHUNKS:
                 load_chunk(c + RAW_BUFS)
 
+        def w_operand(c, t, g):
+            codes, scales = w_packed_of[c]
+            tile = t * CHUNK_PASSES + g
+            return codes[:, tile * P : (tile + 1) * P], scales[:, tile * STAGGER : tile * STAGGER + P]
+
         def quantise_w(c, tiles):
             if tiles[0] == 0:
                 w_codes = stage.tile([P, W_CODES_START + TILE_COLS * ROW_TILES], U32, bufs=2, align_bytes=STAGGER)
-                w_scales = stage.tile([P, W_SCALES_START + TILE_COLS * ROW_TILES], U8, bufs=2, align_bytes=STAGGER)
-                w_packed_of[c] = (w_codes[:, W_CODES_START:], w_scales[:, W_SCALES_START:])
-            codes, scales = w_packed_of[c]
-            for t in tiles:
-                cols = slice(t * TILE_COLS, (t + 1) * TILE_COLS)
-                nc.vector.quantize_mx(
-                    out=codes[:, cols].bitcast(FP8X4), scales=scales[:, cols], in_=w_grouped_of[c][:, t, :]
+                w_scales = stage.tile(
+                    [P, W_SCALES_START + STAGGER * CHUNK_PASSES * ROW_TILES], U8, bufs=2, align_bytes=STAGGER
                 )
+                w_packed_of[c] = (w_codes[:, W_CODES_START:], w_scales[:, W_SCALES_START:])
+            for t in tiles:
+                for g in range(CHUNK_PASSES):
+                    codes, scales = w_operand(c, t, g)
+                    nc.vector.quantize_mx(
+                        out=codes.bitcast(FP8X4), scales=scales,
+                        in_=w_grouped_of[c][:, t, g * P * PACK : (g + 1) * P * PACK],
+                    )
 
         def multiply(c, tiles):
-            w_codes, w_scales = w_packed_of[c]
             for t in tiles:
                 for g in range(CHUNK_PASSES):
                     x_codes, x_scales = x_packed_of[c, g]
-                    units = slice(t * TILE_COLS + g * P, t * TILE_COLS + (g + 1) * P)
+                    w_codes, w_scales = w_operand(c, t, g)
                     nc.tensor.matmul_mx(
                         out=acc[t][:],
-                        lhsT=w_codes[:, units].bitcast(FP8X4),
-                        lhsT_scale=w_scales[:, units],
+                        lhsT=w_codes.bitcast(FP8X4),
+                        lhsT_scale=w_scales,
                         rhs=x_codes.bitcast(FP8X4),
                         rhs_scale=x_scales,
                         start=(c == 0 and g == 0),
@@ -208,7 +217,7 @@ def tile_channel_net_pa_k_kernel(tc, x, noise, h, W1, b1, W2, b2, out):
             w2_words = w2_raw[:].bitcast(F32).rearrange("n (p u) -> n u p", u=HALVES)
             w2_flipped = bank_pool.tile([P, HALVES, N_OUT], F32, tag="bank")
             for u in range(HALVES):
-                nc.tensor.transpose(w2_flipped[:, u, :], w2_words[:, u, :], ident[:])
+                nc.tensor.transpose(w2_flipped[:, u, :], w2_words[:, u, :], ident)
             w2_grouped = const.tile([P, N_OUT * PACK], BF16, align_bytes=64)
             nc.scalar.copy(
                 out=w2_grouped[:].bitcast(F32).rearrange("p (c j u) -> p c j u", c=2, u=HALVES),

from contextlib import ExitStack

import concourse.mybir as mybir
from concourse.masks import make_identity

BF16 = mybir.dt.bfloat16
F32 = mybir.dt.float32
U32 = mybir.dt.uint32
U8 = mybir.dt.uint8
FP8X4 = mybir.dt.float8_e4m3fn_x4
ALU = mybir.AluOpType
ACT = mybir.ActivationFunctionType

P = 128
PACK = 4
K_PASS = P * PACK
HALVES = 2

BATCH, K1, HIDDEN, N_OUT = 512, 16384, 512, 128
ROW_TILES = BATCH // P
PASSES = K1 // K_PASS
BANK_TILES = 2
BANK_ROWS = BANK_TILES * P
X_PIECES = ROW_TILES // BANK_TILES

CHUNK_PASSES = 2
CHUNK_K = CHUNK_PASSES * K_PASS
CHUNKS = PASSES // CHUNK_PASSES
PIECED_CHUNKS = (0, 1, CHUNKS - 1)
RAW_BUFS = 8

WARM_START, WARM_X, WARM_W = 4, 2, 1
WARM_COLS = 512

SMALL_CHUNK = CHUNKS - 4

TILE_COLS = CHUNK_PASSES * P
STAGGER = 256
X_SCALES_START = 64
W_CODES_START = 32
W_SCALES_START = 192
IDENT_START = 32

PAIRS = N_OUT // 2
SIDES = 2
SIDE_TILES = ROW_TILES // SIDES
SIDE_ROWS = SIDE_TILES * P

FLOPS = 2 * BATCH * K1 * HIDDEN + 2 * BATCH * HIDDEN * N_OUT


def tile_channel_net_pa_k_kernel(tc, x, noise, h, W1, b1, W2, b2, out):
    nc = tc.nc
    with ExitStack() as ctx:
        ctx.enter_context(tc.manual_schedule())
        const = ctx.enter_context(tc.tile_pool(name="const", bufs=1))
        raw_pool = ctx.enter_context(tc.tile_pool(name="raw", bufs=RAW_BUFS))
        stage = ctx.enter_context(tc.tile_pool(name="stage", bufs=2))
        tail = ctx.enter_context(tc.tile_pool(name="tail", bufs=1))
        acc_pool = ctx.enter_context(tc.psum_pool(name="acc", bufs=1))
        bank_pool = ctx.enter_context(tc.psum_pool(name="bank", bufs=4))

        x_rows = x.rearrange("(p t) k -> p t k", t=ROW_TILES)
        w1_rows = W1.rearrange("(p t) k -> p t k", t=ROW_TILES)

        def load_chunk(c):
            k_range = slice(c * CHUNK_K, (c + 1) * CHUNK_K)
            x_raw = raw_pool.tile([P, ROW_TILES, CHUNK_K], BF16, align_bytes=STAGGER)
            w_raw = raw_pool.tile([P, ROW_TILES, CHUNK_K], BF16, align_bytes=STAGGER)
            x_step, w_step = (BANK_TILES, 1) if c in PIECED_CHUNKS else (ROW_TILES, ROW_TILES)
            for raw, rows, step in ((x_raw, x_rows, x_step), (w_raw, w1_rows, w_step)):
                for t in range(0, ROW_TILES, step):
                    nc.sync.dma_start(out=raw[:, t : t + step, :], in_=rows[:, t : t + step, k_range])
            raw_of[c] = (x_raw, w_raw)

        raw_of = {}
        for c in range(RAW_BUFS):
            load_chunk(c)

        small = const.tile([P, HIDDEN + N_OUT + 2], BF16)
        nc.gpsimd.memset(small[:], 0.0)
        for first, vector in ((0, b1), (HIDDEN, b2), (HIDDEN + N_OUT, h)):
            width = vector.shape[0]
            nc.sync.dma_start(out=small[0:1, first : first + width], in_=vector.rearrange("(o n) -> o n", o=1))
        w2_raw = const.tile([P, HIDDEN], BF16)
        nc.sync.dma_start(out=w2_raw[:], in_=W2)
        noise_sb = const.tile([P, ROW_TILES, N_OUT], BF16)
        nc.sync.dma_start(out=noise_sb[:], in_=noise.rearrange("(p t) n -> p t n", t=ROW_TILES))

        zeros = const.tile([P, WARM_COLS], BF16)
        nc.vector.memset(zeros[:], 0.0)
        one = const.tile([P, 1], F32)
        nc.vector.memset(one[:], 1.0)
        nc.scalar.activation(out=one[:], in_=one[:], func=ACT.Sqrt)

        ident_tile = const.tile([P, IDENT_START + P], F32, align_bytes=STAGGER)
        ident = ident_tile[:, IDENT_START:]
        make_identity(nc, ident)
        ones = const.tile([P, P], BF16)
        nc.vector.memset(ones[:], 1.0)
        b1_f = const.tile([P, PACK], F32)
        b2_planes = const.tile([P, N_OUT], F32)
        h_f = const.tile([P, 2], F32)
        minus_h1 = const.tile([P, 1], F32)

        def spread_small_vectors():
            spread = bank_pool.tile([P, PACK + N_OUT + 2], F32, tag="bank")
            for t in range(PACK):
                nc.tensor.matmul(
                    spread[:, t : t + 1], lhsT=small[:, t:HIDDEN:PACK], rhs=ones[:, 0:1], start=True, stop=True
                )
            nc.tensor.matmul(spread[:, PACK:], lhsT=ones[:], rhs=small[:, HIDDEN:], start=True, stop=True)
            nc.scalar.copy(out=b1_f[:], in_=spread[:, :PACK])
            nc.scalar.copy(
                out=b2_planes[:].rearrange("p (c j) -> p c j", c=2),
                in_=spread[:, PACK : PACK + N_OUT].rearrange("p (j c) -> p c j", c=2),
            )
            nc.scalar.copy(out=h_f[:], in_=spread[:, PACK + N_OUT :])
            nc.scalar.mul(minus_h1[:], spread[:, PACK + N_OUT + 1 :], -1.0)

        acc = [acc_pool.tile([P, BATCH], F32, name="acc%d" % t) for t in range(PACK)]

        def transpose_words(out, raw, row_tile, first_word):
            words = raw[:].bitcast(F32)[:, row_tile, first_word : first_word + P]
            nc.tensor.transpose(out, words, ident)

        def empty_bank(first, out, in_):
            copy = nc.vector.tensor_copy if first else nc.scalar.copy
            copy(out=out, in_=in_)

        x_grouped_of, x_packed_of, w_grouped_of, w_packed_of = {}, {}, {}, {}

        def flip_x(c, piece):
            for g in range(CHUNK_PASSES):
                if piece == 0:
                    x_grouped = stage.tile([P, BATCH * PACK], BF16, bufs=4, align_bytes=64)
                    x_grouped_of[c, g] = x_grouped
                flipped = bank_pool.tile([P, HALVES, BANK_ROWS], F32, tag="bank")
                for local in range(BANK_TILES):
                    for u in range(HALVES):
                        transpose_words(
                            flipped[:, u, local * P : (local + 1) * P],
                            raw_of[c][0], piece * BANK_TILES + local, (g * HALVES + u) * P,
                        )
                grouped_words = x_grouped_of[c, g][:].bitcast(F32).rearrange("p (r u) -> p r u", u=HALVES)
                empty_bank(
                    piece == 0 and g == 0,
                    grouped_words[:, piece * BANK_ROWS : (piece + 1) * BANK_ROWS, :],
                    flipped[:].rearrange("p u r -> p r u"),
                )

        def quantise_x(c):
            for g in range(CHUNK_PASSES):
                x_codes = stage.tile([P, BATCH], U32, bufs=4, align_bytes=STAGGER)
                x_scales = stage.tile([P, X_SCALES_START + BATCH], U8, bufs=4, align_bytes=STAGGER)
                x_packed_of[c, g] = (x_codes[:], x_scales[:, X_SCALES_START:])
                nc.vector.quantize_mx(
                    out=x_codes[:].bitcast(FP8X4), scales=x_scales[:, X_SCALES_START:], in_=x_grouped_of[c, g][:]
                )

        def flip_w(c, t, on_vector):
            if t == 0:
                w_grouped = stage.tile([P, ROW_TILES, CHUNK_PASSES * P * PACK], BF16, bufs=2, align_bytes=64)
                w_grouped_of[c] = w_grouped
            flipped = bank_pool.tile([P, CHUNK_PASSES, HALVES, P], F32, tag="bank")
            for g in range(CHUNK_PASSES):
                for u in range(HALVES):
                    transpose_words(flipped[:, g, u, :], raw_of[c][1], t, (g * HALVES + u) * P)
            empty_bank(
                on_vector,
                w_grouped_of[c][:, t, :].bitcast(F32).rearrange("p (g r u) -> p g r u", g=CHUNK_PASSES, u=HALVES),
                flipped[:].rearrange("p g u r -> p g r u"),
            )
            if t == ROW_TILES - 1 and c + RAW_BUFS < CHUNKS:
                load_chunk(c + RAW_BUFS)

        def w_operand(c, t, g):
            codes, scales = w_packed_of[c]
            tile = t * CHUNK_PASSES + g
            return codes[:, tile * P : (tile + 1) * P], scales[:, tile * STAGGER : tile * STAGGER + P]

        def quantise_w(c, tiles):
            if tiles[0] == 0:
                w_codes = stage.tile([P, W_CODES_START + TILE_COLS * ROW_TILES], U32, bufs=2, align_bytes=STAGGER)
                w_scales = stage.tile(
                    [P, W_SCALES_START + STAGGER * CHUNK_PASSES * ROW_TILES], U8, bufs=2, align_bytes=STAGGER
                )
                w_packed_of[c] = (w_codes[:, W_CODES_START:], w_scales[:, W_SCALES_START:])
            for t in tiles:
                for g in range(CHUNK_PASSES):
                    codes, scales = w_operand(c, t, g)
                    nc.vector.quantize_mx(
                        out=codes.bitcast(FP8X4), scales=scales,
                        in_=w_grouped_of[c][:, t, g * P * PACK : (g + 1) * P * PACK],
                    )

        def multiply(c, tiles):
            for t in tiles:
                for g in range(CHUNK_PASSES):
                    x_codes, x_scales = x_packed_of[c, g]
                    w_codes, w_scales = w_operand(c, t, g)
                    nc.tensor.matmul_mx(
                        out=acc[t][:],
                        lhsT=w_codes.bitcast(FP8X4),
                        lhsT_scale=w_scales,
                        rhs=x_codes.bitcast(FP8X4),
                        rhs_scale=x_scales,
                        start=(c == 0 and g == 0),
                        stop=(c == CHUNKS - 1 and g == CHUNK_PASSES - 1),
                    )

        def keep_warm(count):
            for i in range(count):
                nc.tensor.matmul(acc[0][:], lhsT=zeros[:, :P], rhs=zeros[:], start=True, stop=True)

        def flip_w2():
            w2_words = w2_raw[:].bitcast(F32).rearrange("n (p u) -> n u p", u=HALVES)
            w2_flipped = bank_pool.tile([P, HALVES, N_OUT], F32, tag="bank")
            for u in range(HALVES):
                nc.tensor.transpose(w2_flipped[:, u, :], w2_words[:, u, :], ident)
            w2_grouped = const.tile([P, N_OUT * PACK], BF16, align_bytes=64)
            nc.scalar.copy(
                out=w2_grouped[:].bitcast(F32).rearrange("p (c j u) -> p c j u", c=2, u=HALVES),
                in_=w2_flipped[:].rearrange("p u (j c) -> p c j u", c=2),
            )
            return w2_grouped

        def quantise_w2(w2_grouped):
            w2_codes = const.tile([P, N_OUT], U32, align_bytes=64)
            w2_scales = const.tile([P, N_OUT], U8, align_bytes=64)
            nc.vector.quantize_mx(out=w2_codes[:].bitcast(FP8X4), scales=w2_scales[:], in_=w2_grouped[:])
            return w2_codes, w2_scales

        keep_warm(WARM_START)
        for c in range(CHUNKS - 1):
            for piece in range(X_PIECES):
                flip_x(c, piece)
                if c == 0:
                    keep_warm(WARM_X)
            if c > 0:
                multiply(c - 1, [0, 1])
            quantise_x(c)
            for t in range(ROW_TILES):
                flip_w(c, t, t == 0)
                if c == 0:
                    keep_warm(WARM_W)
            if c == SMALL_CHUNK:
                w2_grouped = flip_w2()
                spread_small_vectors()
            if c > 0:
                multiply(c - 1, [2, 3])
            quantise_w(c, range(ROW_TILES))
            if c == SMALL_CHUNK:
                w2_codes, w2_scales = quantise_w2(w2_grouped)
        last = CHUNKS - 1
        for piece in range(X_PIECES):
            flip_x(last, piece)
        multiply(last - 1, [0, 1, 2])
        quantise_x(last)
        for t in range(ROW_TILES):
            flip_w(last, t, False)
            quantise_w(last, [t])
        multiply(last - 1, [3])
        multiply(last, range(ROW_TILES))

        a_planes = tail.tile([P, PACK, BATCH], BF16)

        def relu_on_vector(t, first, last):
            nc.vector.tensor_scalar(
                out=a_planes[:, t, first:last], in0=acc[t][:, first:last], scalar1=b1_f[:, t : t + 1], scalar2=0.0,
                op0=ALU.add, op1=ALU.max,
            )

        def relu_on_scalar(t, first, last):
            nc.scalar.activation(
                out=a_planes[:, t, first:last], in_=acc[t][:, first:last], func=ACT.Relu,
                bias=b1_f[:, t : t + 1], scale=1.0,
            )

        relu_on_scalar(0, 0, BATCH)
        relu_on_vector(1, 0, BATCH)
        relu_on_scalar(2, 0, BATCH)
        relu_on_vector(3, 0, SIDE_ROWS)
        relu_on_scalar(3, SIDE_ROWS, BATCH)

        a_grouped = tail.tile([P, BATCH, PACK], BF16, align_bytes=64)

        def group_columns(copy, first, last):
            copy(out=a_grouped[:, first:last, :], in_=a_planes[:, :, first:last].rearrange("p t b -> p b t"))

        group_columns(nc.vector.tensor_copy, 0, SIDE_ROWS)
        group_columns(nc.vector.tensor_copy, SIDE_ROWS, SIDE_ROWS + P)
        group_columns(nc.scalar.copy, SIDE_ROWS + P, BATCH)

        a_codes = tail.tile([P, BATCH], U32, align_bytes=64)
        a_scales = tail.tile([P, BATCH], U8, align_bytes=64)
        a_flat = a_grouped[:].rearrange("p b t -> p (b t)")
        z = tail.tile([P, ROW_TILES, N_OUT], F32)
        for side in range(SIDES):
            cols = slice(side * SIDE_ROWS, (side + 1) * SIDE_ROWS)
            nc.vector.quantize_mx(
                out=a_codes[:, cols].bitcast(FP8X4),
                scales=a_scales[:, cols],
                in_=a_flat[:, side * SIDE_ROWS * PACK : (side + 1) * SIDE_ROWS * PACK],
            )
        for side in range(SIDES):
            z_ps = bank_pool.tile([P, SIDE_TILES, N_OUT], F32, tag="bank")
            for local in range(SIDE_TILES):
                t = side * SIDE_TILES + local
                rows = slice(t * P, (t + 1) * P)
                nc.tensor.matmul_mx(
                    out=z_ps[:, local, :],
                    lhsT=a_codes[:, rows].bitcast(FP8X4),
                    lhsT_scale=a_scales[:, rows],
                    rhs=w2_codes[:].bitcast(FP8X4),
                    rhs_scale=w2_scales[:],
                    start=True,
                    stop=True,
                )
            nc.vector.tensor_tensor(
                out=z[:, side * SIDE_TILES : (side + 1) * SIDE_TILES, :],
                in0=z_ps[:],
                in1=b2_planes[:].unsqueeze(1).to_broadcast([P, SIDE_TILES, N_OUT]),
                op=ALU.add,
            )

        squares = tail.tile([P, ROW_TILES, N_OUT], F32)
        sum_sq = tail.tile([P, ROW_TILES], F32)
        for t in range(ROW_TILES):
            nc.scalar.activation(
                out=squares[:, t, :], in_=z[:, t, :], func=ACT.Square, accum_out=sum_sq[:, t : t + 1]
            )
        norm_by_8 = tail.tile([P, ROW_TILES], F32)
        nc.scalar.activation(out=norm_by_8[:], in_=sum_sq[:], func=ACT.Sqrt, scale=1.0 / PAIRS)

        z_h0 = tail.tile([P, ROW_TILES, N_OUT], F32)
        turned = tail.tile([P, ROW_TILES, N_OUT], F32)
        nc.vector.tensor_scalar(out=z_h0[:], in0=z[:], scalar1=h_f[:, 0:1], scalar2=None, op0=ALU.mult)
        z_planes = z[:].rearrange("p t (c j) -> p t c j", c=2)
        z_h0_planes = z_h0[:].rearrange("p t (c j) -> p t c j", c=2)
        turned_planes = turned[:].rearrange("p t (c j) -> p t c j", c=2)
        nc.vector.scalar_tensor_tensor(
            out=turned_planes[:, :, 0, :], in0=z_planes[:, :, 1, :], scalar=minus_h1[:, 0:1],
            in1=z_h0_planes[:, :, 0, :], op0=ALU.mult, op1=ALU.add,
        )
        nc.vector.scalar_tensor_tensor(
            out=turned_planes[:, :, 1, :], in0=z_planes[:, :, 0, :], scalar=h_f[:, 1:2],
            in1=z_h0_planes[:, :, 1, :], op0=ALU.mult, op1=ALU.add,
        )

        gain = tail.tile([P, ROW_TILES], F32)
        nc.vector.reciprocal(out=gain[:], in_=norm_by_8[:])
        y = tail.tile([P, ROW_TILES, N_OUT], F32)
        out_rows = out.rearrange("(p t) n -> p t n", t=ROW_TILES)
        for side in range(SIDES):
            tiles = slice(side * SIDE_TILES, (side + 1) * SIDE_TILES)
            for t in range(side * SIDE_TILES, (side + 1) * SIDE_TILES):
                nc.vector.scalar_tensor_tensor(
                    out=y[:, t, :].rearrange("p (j c) -> p j c", c=2),
                    in0=turned_planes[:, t, :, :].rearrange("p c j -> p j c"),
                    scalar=gain[:, t : t + 1],
                    in1=noise_sb[:, t, :].rearrange("p (j c) -> p j c", c=2),
                    op0=ALU.mult,
                    op1=ALU.add,
                )
            nc.sync.dma_start(out=out_rows[:, tiles, :], in_=y[:, tiles, :])
